import numpy as np
import ml_dtypes

BF16 = ml_dtypes.bfloat16


def bf(x):
    return np.asarray(x, np.float32).astype(BF16)


def f32(x):
    return np.asarray(x, np.float32)


def f64(x):
    return np.asarray(x).astype(np.float64)


def striped(idx):
    return np.tile(idx.reshape(-1, 16).T, (8, 1))


C, S, H, K, N, E, Q, U, R = 256, 512, 256, 4, 1024, 512, 16, 128, 4

GATE_COEF = np.array([[0, 0, 0, 0], [0, 0, 0, 1], [0, 1, 0, -1], [0, 1, 0, 0], [0, 0, 1, -1], [0, 0, 1, 0], [0, 1, 1, -2], [0, 1, 1, -1], [1, -1, -1, 1], [1, -1, -1, 2], [1, 0, -1, 0], [1, 0, -1, 1], [1, -1, 0, 0], [1, -1, 0, 1], [1, 0, 0, -1], [1, 0, 0, 0]], np.float64)


def setup_inputs():
    return {"x": f32(np.random.random((C, S))), "w": f32(2.0 * np.random.standard_normal((Q, E))), "offs": striped(np.concatenate([np.random.permutation(S)[:H] for _ in range(K)]))}


def reference(x, w, offs):
    idx = offs[:16].T.reshape(-1)
    ia, ib = idx[:E], idx[E:]
    e = np.exp(f64(w))
    p = e / e.sum(axis=0, keepdims=True)
    coef = (GATE_COEF[:, :, None] * p[:, None, :]).sum(axis=0)
    a = f64(x)[:, ia]
    b = f64(x)[:, ib]
    h = coef[0] + coef[1] * a + coef[2] * b + coef[3] * (a * b)
    return h.reshape(C, U, R).sum(axis=-1)

@@ -1,0 +1,119 @@
+import concourse.mybir as mybir
+from concourse.masks import make_identity
+
+F32 = mybir.dt.float32
+U16 = mybir.dt.uint16
+ALU = mybir.AluOpType
+ACT = mybir.ActivationFunctionType
+AX = mybir.AxisListType
+
+P = 128
+SAMPLES, SIGNALS = 256, 512
+GATES, NEURONS = 16, 512
+GROUP = 4
+CLASSES = NEURONS // GROUP
+BLOCKS = SAMPLES // P
+CHUNKS = NEURONS // P
+LIST_COLS = NEURONS // 16
+
+
+def tile_logicgatenetwork_kernel(tc, x, w, offs, out):
+    nc = tc.nc
+    with (
+        tc.tile_pool(name="held", bufs=1) as held,
+        tc.tile_pool(name="work", bufs=2) as work,
+        tc.psum_pool(name="psum", bufs=1) as psum,
+    ):
+        offsets = held.tile([P, 2 * LIST_COLS], U16, name="offsets")
+        nc.sync.dma_start(offsets[:], offs)
+        logits = held.tile([CHUNKS * GATES, P], F32, name="logits")
+        for c in range(CHUNKS):
+            nc.scalar.dma_start(logits[c * GATES : (c + 1) * GATES, :], w[:, c * P : (c + 1) * P])
+        signals = [held.tile([P, SIGNALS], F32, name=f"signals{b}") for b in range(BLOCKS)]
+        for b in range(BLOCKS):
+            nc.sync.dma_start(signals[b][:], x[b * P : (b + 1) * P, :])
+
+        ident = held.tile([P, P], F32, name="ident")
+        make_identity(nc, ident[:])
+        ones = held.tile([P, P], F32, name="ones")
+        nc.vector.memset(ones[:], 1.0)
+        group_of = held.tile([P, P // GROUP], F32, name="group_of")
+        nc.vector.reduce_sum(group_of[:], ident[:].rearrange("p (v r) -> p v r", r=GROUP), axis=AX.X)
+        truth = held.tile([P, 4, GATES], F32, name="truth")
+        nc.vector.memset(truth[:], 0.0)
+        for i in range(4):
+            period = GATES >> i
+            upper_half = truth[:, i, :].rearrange("p (n s) -> p n s", s=period)[:, :, period // 2 :]
+            nc.vector.memset(upper_half, 1.0)
+        gate_poly = held.tile([P, 5, GATES], F32, name="gate_poly")
+        nc.vector.memset(gate_poly[:, 0, :], 1.0)
+        nc.vector.tensor_copy(gate_poly[:, 1, :], truth[:, 0, :])
+        nc.vector.tensor_sub(gate_poly[:, 2, :], truth[:, 2, :], truth[:, 0, :])
+        nc.vector.tensor_sub(gate_poly[:, 3, :], truth[:, 1, :], truth[:, 0, :])
+        nc.vector.tensor_sub(gate_poly[:, 4, :], truth[:, 3, :], truth[:, 2, :])
+        nc.vector.tensor_sub(gate_poly[:, 4, :], gate_poly[:, 4, :], gate_poly[:, 3, :])
+
+        logits_t = psum.tile([P, CHUNKS, GATES], F32, name="logits_t")
+        nc.tensor.transpose(
+            logits_t[:].rearrange("p c q -> p (c q)"), logits[:], ident[: CHUNKS * GATES, : CHUNKS * GATES]
+        )
+        top = held.tile([P, CHUNKS], F32, name="top")
+        nc.vector.reduce_max(top[:], logits_t[:], axis=AX.X)
+        shifted = held.tile([P, CHUNKS, GATES], F32, name="shifted")
+        nc.vector.tensor_tensor(
+            shifted[:], logits_t[:], top[:].unsqueeze(2).to_broadcast([P, CHUNKS, GATES]), ALU.subtract
+        )
+        expw = held.tile([P, CHUNKS, GATES], F32, name="expw")
+        nc.scalar.activation(expw[:], shifted[:], ACT.Exp)
+        weighted = held.tile([P, 5, CHUNKS, GATES], F32, name="weighted")
+        nc.vector.tensor_tensor(
+            weighted[:],
+            expw[:].unsqueeze(1).to_broadcast([P, 5, CHUNKS, GATES]),
+            gate_poly[:].unsqueeze(2).to_broadcast([P, 5, CHUNKS, GATES]),
+            ALU.mult,
+        )
+        sums = held.tile([P, 5, CHUNKS], F32, name="sums")
+        nc.vector.reduce_sum(sums[:], weighted[:], axis=AX.X)
+        inv = held.tile([P, CHUNKS], F32, name="inv")
+        nc.vector.reciprocal(inv[:], sums[:, 0, :])
+        coef = held.tile([P, 4, CHUNKS], F32, name="coef")
+        nc.vector.tensor_tensor(
+            coef[:], sums[:, 1:5, :], inv[:].unsqueeze(1).to_broadcast([P, 4, CHUNKS]), ALU.mult
+        )
+
+        def as_rows(k, name):
+            bank = psum.tile([P, NEURONS], F32, name="bank_" + name)
+            for c in range(CHUNKS):
+                nc.tensor.transpose(bank[:, c * P : (c + 1) * P], coef[:, k, c : c + 1].to_broadcast([P, P]), ident[:])
+            rows = held.tile([P, NEURONS], F32, name="rows_" + name)
+            nc.scalar.copy(rows[:], bank[:])
+            return rows
+
+        rows_ta = as_rows(1, "ta")
+        rows_tab = as_rows(3, "tab")
+        rows_tb = as_rows(2, "tb")
+        t0_spread = held.tile([P, CHUNKS, P // GROUP], F32, name="t0_spread")
+        nc.vector.tensor_tensor(
+            t0_spread[:],
+            group_of[:].unsqueeze(1).to_broadcast([P, CHUNKS, P // GROUP]),
+            coef[:, 0, :].unsqueeze(2).to_broadcast([P, CHUNKS, P // GROUP]),
+            ALU.mult,
+        )
+        t0_sum = psum.tile([P, CLASSES], F32, name="t0_sum")
+        nc.tensor.matmul(t0_sum[:], ones[:], t0_spread[:].rearrange("p c v -> p (c v)"), start=True, stop=True)
+
+        list_a = offsets[:, 0:LIST_COLS]
+        list_b = offsets[:, LIST_COLS : 2 * LIST_COLS]
+        for b in range(BLOCKS):
+            lin_a = work.tile([P, NEURONS], F32, name="lin_a")
+            nc.vector.tensor_tensor(lin_a[:], signals[b][:].indirect(list_a), rows_ta[:], ALU.mult)
+            slope_b = work.tile([P, NEURONS], F32, name="slope_b")
+            nc.vector.tensor_tensor(slope_b[:], signals[b][:].indirect(list_a), rows_tab[:], ALU.mult)
+            nc.vector.tensor_tensor(slope_b[:], slope_b[:], rows_tb[:], ALU.add)
+            h = work.tile([P, NEURONS], F32, name="h")
+            nc.vector.tensor_tensor(h[:], signals[b][:].indirect(list_b), slope_b[:], ALU.mult)
+            nc.vector.tensor_tensor(h[:], h[:], lin_a[:], ALU.add)
+            score = work.tile([P, CLASSES], F32, name="score")
+            nc.vector.reduce_sum(score[:], h[:].rearrange("p (u r) -> p u r", r=GROUP), axis=AX.X)
+            nc.vector.tensor_tensor(score[:], score[:], t0_sum[:], ALU.add)
+            nc.sync.dma_start(out[b * P : (b + 1) * P, :], score[:])

@@ -21,17 +21,19 @@ def tile_logicgatenetwork_kernel(tc, x, w, offs, out):
     nc = tc.nc
     with (
         tc.tile_pool(name="held", bufs=1) as held,
-        tc.tile_pool(name="work", bufs=2) as work,
         tc.psum_pool(name="psum", bufs=1) as psum,
     ):
-        offsets = held.tile([P, 2 * LIST_COLS], U16, name="offsets")
-        nc.sync.dma_start(offsets[:], offs)
         logits = held.tile([CHUNKS * GATES, P], F32, name="logits")
         for c in range(CHUNKS):
-            nc.scalar.dma_start(logits[c * GATES : (c + 1) * GATES, :], w[:, c * P : (c + 1) * P])
+            nc.sync.dma_start(logits[c * GATES : (c + 1) * GATES, :], w[:, c * P : (c + 1) * P])
+        offsets = held.tile([P, 2 * LIST_COLS], U16, name="offsets")
+        nc.sync.dma_start(offsets[:], offs)
         signals = [held.tile([P, SIGNALS], F32, name=f"signals{b}") for b in range(BLOCKS)]
         for b in range(BLOCKS):
             nc.sync.dma_start(signals[b][:], x[b * P : (b + 1) * P, :])
+        warm = held.tile([P, 1], F32, name="warm")
+        nc.vector.memset(warm[:], 0.0)
+        nc.scalar.activation(warm[:], warm[:], ACT.Exp)
 
         ident = held.tile([P, P], F32, name="ident")
         make_identity(nc, ident[:])
@@ -45,13 +47,12 @@ def tile_logicgatenetwork_kernel(tc, x, w, offs, out):
             period = GATES >> i
             upper_half = truth[:, i, :].rearrange("p (n s) -> p n s", s=period)[:, :, period // 2 :]
             nc.vector.memset(upper_half, 1.0)
-        gate_poly = held.tile([P, 5, GATES], F32, name="gate_poly")
-        nc.vector.memset(gate_poly[:, 0, :], 1.0)
-        nc.vector.tensor_copy(gate_poly[:, 1, :], truth[:, 0, :])
-        nc.vector.tensor_sub(gate_poly[:, 2, :], truth[:, 2, :], truth[:, 0, :])
-        nc.vector.tensor_sub(gate_poly[:, 3, :], truth[:, 1, :], truth[:, 0, :])
-        nc.vector.tensor_sub(gate_poly[:, 4, :], truth[:, 3, :], truth[:, 2, :])
-        nc.vector.tensor_sub(gate_poly[:, 4, :], gate_poly[:, 4, :], gate_poly[:, 3, :])
+        gate_poly = held.tile([P, 4, GATES], F32, name="gate_poly")
+        nc.vector.tensor_copy(gate_poly[:, 0, :], truth[:, 0, :])
+        nc.vector.tensor_sub(gate_poly[:, 1, :], truth[:, 2, :], truth[:, 0, :])
+        nc.vector.tensor_sub(gate_poly[:, 2, :], truth[:, 1, :], truth[:, 0, :])
+        nc.vector.tensor_sub(gate_poly[:, 3, :], truth[:, 3, :], truth[:, 2, :])
+        nc.vector.tensor_sub(gate_poly[:, 3, :], gate_poly[:, 3, :], gate_poly[:, 2, :])
 
         logits_t = psum.tile([P, CHUNKS, GATES], F32, name="logits_t")
         nc.tensor.transpose(
@@ -65,21 +66,21 @@ def tile_logicgatenetwork_kernel(tc, x, w, offs, out):
         )
         expw = held.tile([P, CHUNKS, GATES], F32, name="expw")
         nc.scalar.activation(expw[:], shifted[:], ACT.Exp)
-        weighted = held.tile([P, 5, CHUNKS, GATES], F32, name="weighted")
+        weighted = held.tile([P, 4, CHUNKS, GATES], F32, name="weighted")
         nc.vector.tensor_tensor(
             weighted[:],
-            expw[:].unsqueeze(1).to_broadcast([P, 5, CHUNKS, GATES]),
-            gate_poly[:].unsqueeze(2).to_broadcast([P, 5, CHUNKS, GATES]),
+            expw[:].unsqueeze(1).to_broadcast([P, 4, CHUNKS, GATES]),
+            gate_poly[:].unsqueeze(2).to_broadcast([P, 4, CHUNKS, GATES]),
             ALU.mult,
         )
-        sums = held.tile([P, 5, CHUNKS], F32, name="sums")
+        denom = held.tile([P, CHUNKS], F32, name="denom")
+        nc.vector.reduce_sum(denom[:], expw[:], axis=AX.X)
+        sums = held.tile([P, 4, CHUNKS], F32, name="sums")
         nc.vector.reduce_sum(sums[:], weighted[:], axis=AX.X)
         inv = held.tile([P, CHUNKS], F32, name="inv")
-        nc.vector.reciprocal(inv[:], sums[:, 0, :])
+        nc.vector.reciprocal(inv[:], denom[:])
         coef = held.tile([P, 4, CHUNKS], F32, name="coef")
-        nc.vector.tensor_tensor(
-            coef[:], sums[:, 1:5, :], inv[:].unsqueeze(1).to_broadcast([P, 4, CHUNKS]), ALU.mult
-        )
+        nc.vector.tensor_tensor(coef[:], sums[:], inv[:].unsqueeze(1).to_broadcast([P, 4, CHUNKS]), ALU.mult)
 
         def as_rows(k, name):
             bank = psum.tile([P, NEURONS], F32, name="bank_" + name)
@@ -99,21 +100,32 @@ def tile_logicgatenetwork_kernel(tc, x, w, offs, out):
             coef[:, 0, :].unsqueeze(2).to_broadcast([P, CHUNKS, P // GROUP]),
             ALU.mult,
         )
-        t0_sum = psum.tile([P, CLASSES], F32, name="t0_sum")
-        nc.tensor.matmul(t0_sum[:], ones[:], t0_spread[:].rearrange("p c v -> p (c v)"), start=True, stop=True)
 
         list_a = offsets[:, 0:LIST_COLS]
         list_b = offsets[:, LIST_COLS : 2 * LIST_COLS]
+
+        def per_block(name, columns):
+            return [held.tile([P, columns], F32, name=f"{name}{b}") for b in range(BLOCKS)]
+
+        lin_a = per_block("lin_a", NEURONS)
+        part = [psum.tile([P, CLASSES], F32, name=f"part{b}") for b in range(BLOCKS)]
         for b in range(BLOCKS):
-            lin_a = work.tile([P, NEURONS], F32, name="lin_a")
-            nc.vector.tensor_tensor(lin_a[:], signals[b][:].indirect(list_a), rows_ta[:], ALU.mult)
-            slope_b = work.tile([P, NEURONS], F32, name="slope_b")
-            nc.vector.tensor_tensor(slope_b[:], signals[b][:].indirect(list_a), rows_tab[:], ALU.mult)
-            nc.vector.tensor_tensor(slope_b[:], slope_b[:], rows_tb[:], ALU.add)
-            h = work.tile([P, NEURONS], F32, name="h")
-            nc.vector.tensor_tensor(h[:], signals[b][:].indirect(list_b), slope_b[:], ALU.mult)
-            nc.vector.tensor_tensor(h[:], h[:], lin_a[:], ALU.add)
-            score = work.tile([P, CLASSES], F32, name="score")
-            nc.vector.reduce_sum(score[:], h[:].rearrange("p (u r) -> p u r", r=GROUP), axis=AX.X)
-            nc.vector.tensor_tensor(score[:], score[:], t0_sum[:], ALU.add)
-            nc.sync.dma_start(out[b * P : (b + 1) * P, :], score[:])
+            nc.vector.tensor_tensor(lin_a[b][:], signals[b][:].indirect(list_a), rows_ta[:], ALU.mult)
+            nc.tensor.matmul(part[b][:], ones[:], t0_spread[:].rearrange("p c v -> p (c v)"), start=True, stop=False)
+            by_group = lin_a[b][:].rearrange("p (u r) -> p u r", r=GROUP)
+            for r in range(GROUP):
+                nc.tensor.matmul(part[b][:], ident[:], by_group[:, :, r], start=False, stop=r == GROUP - 1)
+        slope_b = per_block("slope_b", NEURONS)
+        for b in range(BLOCKS):
+            nc.vector.tensor_tensor(slope_b[b][:], signals[b][:].indirect(list_a), rows_tab[:], ALU.mult)
+        for b in range(BLOCKS):
+            nc.vector.tensor_tensor(slope_b[b][:], slope_b[b][:], rows_tb[:], ALU.add)
+        with_b = per_block("with_b", NEURONS)
+        for b in range(BLOCKS):
+            nc.vector.tensor_tensor(with_b[b][:], signals[b][:].indirect(list_b), slope_b[b][:], ALU.mult)
+        score = per_block("score", CLASSES)
+        for b in range(BLOCKS):
+            nc.vector.reduce_sum(score[b][:], with_b[b][:].rearrange("p (u r) -> p u r", r=GROUP), axis=AX.X)
+        for b in range(BLOCKS):
+            nc.vector.tensor_tensor(score[b][:], score[b][:], part[b][:], ALU.add)
+            nc.sync.dma_start(out[b * P : (b + 1) * P, :], score[b][:])

@@ -14,7 +14,11 @@ GROUP = 4
 CLASSES = NEURONS // GROUP
 BLOCKS = SAMPLES // P
 CHUNKS = NEURONS // P
-LIST_COLS = NEURONS // 16
+PIECE = 256
+PIECES = NEURONS // PIECE
+PIECE_COLS = PIECE // 16
+PIECE_CHUNKS = PIECE // P
+PIECE_CLASSES = PIECE // GROUP
 
 
 def tile_logicgatenetwork_kernel(tc, x, w, offs, out):
@@ -22,11 +26,12 @@ def tile_logicgatenetwork_kernel(tc, x, w, offs, out):
     with (
         tc.tile_pool(name="held", bufs=1) as held,
         tc.psum_pool(name="psum", bufs=1) as psum,
+        tc.psum_pool(name="row_banks", bufs=3) as row_banks,
     ):
         logits = held.tile([CHUNKS * GATES, P], F32, name="logits")
         for c in range(CHUNKS):
             nc.sync.dma_start(logits[c * GATES : (c + 1) * GATES, :], w[:, c * P : (c + 1) * P])
-        offsets = held.tile([P, 2 * LIST_COLS], U16, name="offsets")
+        offsets = held.tile([P, 2 * PIECES * PIECE_COLS], U16, name="offsets")
         nc.sync.dma_start(offsets[:], offs)
         signals = [held.tile([P, SIGNALS], F32, name=f"signals{b}") for b in range(BLOCKS)]
         for b in range(BLOCKS):
@@ -83,11 +88,15 @@ def tile_logicgatenetwork_kernel(tc, x, w, offs, out):
         nc.vector.tensor_tensor(coef[:], sums[:], inv[:].unsqueeze(1).to_broadcast([P, 4, CHUNKS]), ALU.mult)
 
         def as_rows(k, name):
-            bank = psum.tile([P, NEURONS], F32, name="bank_" + name)
-            for c in range(CHUNKS):
-                nc.tensor.transpose(bank[:, c * P : (c + 1) * P], coef[:, k, c : c + 1].to_broadcast([P, P]), ident[:])
-            rows = held.tile([P, NEURONS], F32, name="rows_" + name)
-            nc.scalar.copy(rows[:], bank[:])
+            rows = [held.tile([P, PIECE], F32, name=f"rows_{name}{piece}") for piece in range(PIECES)]
+            for piece in range(PIECES):
+                bank = row_banks.tile([P, PIECE], F32, name="bank")
+                for i in range(PIECE_CHUNKS):
+                    c = piece * PIECE_CHUNKS + i
+                    nc.tensor.transpose(
+                        bank[:, i * P : (i + 1) * P], coef[:, k, c : c + 1].to_broadcast([P, P]), ident[:]
+                    )
+                nc.scalar.copy(rows[piece][:], bank[:])
             return rows
 
         rows_ta = as_rows(1, "ta")
@@ -101,31 +110,55 @@ def tile_logicgatenetwork_kernel(tc, x, w, offs, out):
             ALU.mult,
         )
 
-        list_a = offsets[:, 0:LIST_COLS]
-        list_b = offsets[:, LIST_COLS : 2 * LIST_COLS]
+        units = [(piece, b) for piece in range(PIECES) for b in range(BLOCKS)]
 
-        def per_block(name, columns):
-            return [held.tile([P, columns], F32, name=f"{name}{b}") for b in range(BLOCKS)]
+        def picked(b, side, piece):
+            first = (side * PIECES + piece) * PIECE_COLS
+            return signals[b][:].indirect(offsets[:, first : first + PIECE_COLS])
 
-        lin_a = per_block("lin_a", NEURONS)
+        def per_unit(name):
+            return {(piece, b): held.tile([P, PIECE], F32, name=f"{name}{piece}{b}") for piece, b in units}
+
+        def classes_of(tile_of_block, piece):
+            return tile_of_block[:, piece * PIECE_CLASSES : (piece + 1) * PIECE_CLASSES]
+
+        lin_a = per_unit("lin_a")
         part = [psum.tile([P, CLASSES], F32, name=f"part{b}") for b in range(BLOCKS)]
         for b in range(BLOCKS):
-            nc.vector.tensor_tensor(lin_a[b][:], signals[b][:].indirect(list_a), rows_ta[:], ALU.mult)
             nc.tensor.matmul(part[b][:], ones[:], t0_spread[:].rearrange("p c v -> p (c v)"), start=True, stop=False)
-            by_group = lin_a[b][:].rearrange("p (u r) -> p u r", r=GROUP)
+        for piece, b in units:
+            nc.vector.tensor_tensor(lin_a[piece, b][:], picked(b, 0, piece), rows_ta[piece][:], ALU.mult)
+            by_group = lin_a[piece, b][:].rearrange("p (u r) -> p u r", r=GROUP)
             for r in range(GROUP):
-                nc.tensor.matmul(part[b][:], ident[:], by_group[:, :, r], start=False, stop=r == GROUP - 1)
-        slope_b = per_block("slope_b", NEURONS)
-        for b in range(BLOCKS):
-            nc.vector.tensor_tensor(slope_b[b][:], signals[b][:].indirect(list_a), rows_tab[:], ALU.mult)
-        for b in range(BLOCKS):
-            nc.vector.tensor_tensor(slope_b[b][:], slope_b[b][:], rows_tb[:], ALU.add)
-        with_b = per_block("with_b", NEURONS)
-        for b in range(BLOCKS):
-            nc.vector.tensor_tensor(with_b[b][:], signals[b][:].indirect(list_b), slope_b[b][:], ALU.mult)
-        score = per_block("score", CLASSES)
-        for b in range(BLOCKS):
-            nc.vector.reduce_sum(score[b][:], with_b[b][:].rearrange("p (u r) -> p u r", r=GROUP), axis=AX.X)
-        for b in range(BLOCKS):
-            nc.vector.tensor_tensor(score[b][:], score[b][:], part[b][:], ALU.add)
-            nc.sync.dma_start(out[b * P : (b + 1) * P, :], score[b][:])
+                nc.tensor.matmul(
+                    classes_of(part[b], piece),
+                    ident[:],
+                    by_group[:, :, r],
+                    start=False,
+                    stop=piece == PIECES - 1 and r == GROUP - 1,
+                )
+        slope_b = per_unit("slope_b")
+        for piece, b in units:
+            nc.vector.tensor_tensor(slope_b[piece, b][:], picked(b, 0, piece), rows_tab[piece][:], ALU.mult)
+        for piece, b in units:
+            nc.vector.tensor_tensor(slope_b[piece, b][:], slope_b[piece, b][:], rows_tb[piece][:], ALU.add)
+        with_b = per_unit("with_b")
+        score = [held.tile([P, CLASSES], F32, name=f"score{b}") for b in range(BLOCKS)]
+        for step in range(len(units) + 2):
+            if step < len(units):
+                piece, b = units[step]
+                nc.vector.tensor_tensor(with_b[piece, b][:], picked(b, 1, piece), slope_b[piece, b][:], ALU.mult)
+            if 1 <= step <= len(units):
+                piece, b = units[step - 1]
+                nc.vector.reduce_sum(
+                    classes_of(score[b], piece),
+                    with_b[piece, b][:].rearrange("p (u r) -> p u r", r=GROUP),
+                    axis=AX.X,
+                )
+            if step >= 2:
+                piece, b = units[step - 2]
+                nc.vector.tensor_tensor(
+                    classes_of(score[b], piece), classes_of(score[b], piece), classes_of(part[b], piece), ALU.add
+                )
+                if piece == PIECES - 1:
+                    nc.sync.dma_start(out[b * P : (b + 1) * P, :], score[b][:])

@@ -14,11 +14,7 @@ GROUP = 4
 CLASSES = NEURONS // GROUP
 BLOCKS = SAMPLES // P
 CHUNKS = NEURONS // P
-PIECE = 256
-PIECES = NEURONS // PIECE
-PIECE_COLS = PIECE // 16
-PIECE_CHUNKS = PIECE // P
-PIECE_CLASSES = PIECE // GROUP
+LIST_COLS = NEURONS // 16
 
 
 def tile_logicgatenetwork_kernel(tc, x, w, offs, out):
@@ -28,10 +24,9 @@ def tile_logicgatenetwork_kernel(tc, x, w, offs, out):
         tc.psum_pool(name="psum", bufs=1) as psum,
         tc.psum_pool(name="row_banks", bufs=3) as row_banks,
     ):
-        logits = held.tile([CHUNKS * GATES, P], F32, name="logits")
-        for c in range(CHUNKS):
-            nc.sync.dma_start(logits[c * GATES : (c + 1) * GATES, :], w[:, c * P : (c + 1) * P])
-        offsets = held.tile([P, 2 * PIECES * PIECE_COLS], U16, name="offsets")
+        logits = held.tile([GATES * CHUNKS, P], F32, name="logits")
+        nc.sync.dma_start(logits[:], w.rearrange("q (c n) -> (q c) n", c=CHUNKS))
+        offsets = held.tile([P, 2 * LIST_COLS], U16, name="offsets")
         nc.sync.dma_start(offsets[:], offs)
         signals = [held.tile([P, SIGNALS], F32, name=f"signals{b}") for b in range(BLOCKS)]
         for b in range(BLOCKS):
@@ -59,15 +54,14 @@ def tile_logicgatenetwork_kernel(tc, x, w, offs, out):
         nc.vector.tensor_sub(gate_poly[:, 3, :], truth[:, 3, :], truth[:, 2, :])
         nc.vector.tensor_sub(gate_poly[:, 3, :], gate_poly[:, 3, :], gate_poly[:, 2, :])
 
-        logits_t = psum.tile([P, CHUNKS, GATES], F32, name="logits_t")
-        nc.tensor.transpose(
-            logits_t[:].rearrange("p c q -> p (c q)"), logits[:], ident[: CHUNKS * GATES, : CHUNKS * GATES]
-        )
+        logits_t = psum.tile([P, GATES * CHUNKS], F32, name="logits_t")
+        nc.tensor.transpose(logits_t[:], logits[:], ident[: GATES * CHUNKS, : GATES * CHUNKS])
+        by_neuron = logits_t[:].rearrange("p (q c) -> p c q", c=CHUNKS)
         top = held.tile([P, CHUNKS], F32, name="top")
-        nc.vector.reduce_max(top[:], logits_t[:], axis=AX.X)
+        nc.vector.reduce_max(top[:], by_neuron, axis=AX.X)
         shifted = held.tile([P, CHUNKS, GATES], F32, name="shifted")
         nc.vector.tensor_tensor(
-            shifted[:], logits_t[:], top[:].unsqueeze(2).to_broadcast([P, CHUNKS, GATES]), ALU.subtract
+            shifted[:], by_neuron, top[:].unsqueeze(2).to_broadcast([P, CHUNKS, GATES]), ALU.subtract
         )
         expw = held.tile([P, CHUNKS, GATES], F32, name="expw")
         nc.scalar.activation(expw[:], shifted[:], ACT.Exp)
@@ -88,15 +82,14 @@ def tile_logicgatenetwork_kernel(tc, x, w, offs, out):
         nc.vector.tensor_tensor(coef[:], sums[:], inv[:].unsqueeze(1).to_broadcast([P, 4, CHUNKS]), ALU.mult)
 
         def as_rows(k, name):
-            rows = [held.tile([P, PIECE], F32, name=f"rows_{name}{piece}") for piece in range(PIECES)]
-            for piece in range(PIECES):
-                bank = row_banks.tile([P, PIECE], F32, name="bank")
-                for i in range(PIECE_CHUNKS):
-                    c = piece * PIECE_CHUNKS + i
+            rows = held.tile([P, NEURONS], F32, name="rows_" + name)
+            for first in range(0, CHUNKS, 2):
+                bank = row_banks.tile([P, 2 * P], F32, name="bank")
+                for i in range(2):
                     nc.tensor.transpose(
-                        bank[:, i * P : (i + 1) * P], coef[:, k, c : c + 1].to_broadcast([P, P]), ident[:]
+                        bank[:, i * P : (i + 1) * P], coef[:, k, first + i : first + i + 1].to_broadcast([P, P]), ident[:]
                     )
-                nc.scalar.copy(rows[piece][:], bank[:])
+                nc.scalar.copy(rows[:, first * P : (first + 2) * P], bank[:])
             return rows
 
         rows_ta = as_rows(1, "ta")
@@ -110,55 +103,31 @@ def tile_logicgatenetwork_kernel(tc, x, w, offs, out):
             ALU.mult,
         )
 
-        units = [(piece, b) for piece in range(PIECES) for b in range(BLOCKS)]
+        list_a = offsets[:, 0:LIST_COLS]
+        list_b = offsets[:, LIST_COLS : 2 * LIST_COLS]
 
-        def picked(b, side, piece):
-            first = (side * PIECES + piece) * PIECE_COLS
-            return signals[b][:].indirect(offsets[:, first : first + PIECE_COLS])
+        def per_block(name, columns):
+            return [held.tile([P, columns], F32, name=f"{name}{b}") for b in range(BLOCKS)]
 
-        def per_unit(name):
-            return {(piece, b): held.tile([P, PIECE], F32, name=f"{name}{piece}{b}") for piece, b in units}
-
-        def classes_of(tile_of_block, piece):
-            return tile_of_block[:, piece * PIECE_CLASSES : (piece + 1) * PIECE_CLASSES]
-
-        lin_a = per_unit("lin_a")
+        lin_a = per_block("lin_a", NEURONS)
         part = [psum.tile([P, CLASSES], F32, name=f"part{b}") for b in range(BLOCKS)]
         for b in range(BLOCKS):
+            nc.vector.tensor_tensor(lin_a[b][:], signals[b][:].indirect(list_a), rows_ta[:], ALU.mult)
             nc.tensor.matmul(part[b][:], ones[:], t0_spread[:].rearrange("p c v -> p (c v)"), start=True, stop=False)
-        for piece, b in units:
-            nc.vector.tensor_tensor(lin_a[piece, b][:], picked(b, 0, piece), rows_ta[piece][:], ALU.mult)
-            by_group = lin_a[piece, b][:].rearrange("p (u r) -> p u r", r=GROUP)
+            by_group = lin_a[b][:].rearrange("p (u r) -> p u r", r=GROUP)
             for r in range(GROUP):
-                nc.tensor.matmul(
-                    classes_of(part[b], piece),
-                    ident[:],
-                    by_group[:, :, r],
-                    start=False,
-                    stop=piece == PIECES - 1 and r == GROUP - 1,
-                )
-        slope_b = per_unit("slope_b")
-        for piece, b in units:
-            nc.vector.tensor_tensor(slope_b[piece, b][:], picked(b, 0, piece), rows_tab[piece][:], ALU.mult)
-        for piece, b in units:
-            nc.vector.tensor_tensor(slope_b[piece, b][:], slope_b[piece, b][:], rows_tb[piece][:], ALU.add)
-        with_b = per_unit("with_b")
-        score = [held.tile([P, CLASSES], F32, name=f"score{b}") for b in range(BLOCKS)]
-        for step in range(len(units) + 2):
-            if step < len(units):
-                piece, b = units[step]
-                nc.vector.tensor_tensor(with_b[piece, b][:], picked(b, 1, piece), slope_b[piece, b][:], ALU.mult)
-            if 1 <= step <= len(units):
-                piece, b = units[step - 1]
-                nc.vector.reduce_sum(
-                    classes_of(score[b], piece),
-                    with_b[piece, b][:].rearrange("p (u r) -> p u r", r=GROUP),
-                    axis=AX.X,
-                )
-            if step >= 2:
-                piece, b = units[step - 2]
-                nc.vector.tensor_tensor(
-                    classes_of(score[b], piece), classes_of(score[b], piece), classes_of(part[b], piece), ALU.add
-                )
-                if piece == PIECES - 1:
-                    nc.sync.dma_start(out[b * P : (b + 1) * P, :], score[b][:])
+                nc.tensor.matmul(part[b][:], ident[:], by_group[:, :, r], start=False, stop=r == GROUP - 1)
+        slope_b = per_block("slope_b", NEURONS)
+        for b in range(BLOCKS):
+            nc.vector.tensor_tensor(slope_b[b][:], signals[b][:].indirect(list_a), rows_tab[:], ALU.mult)
+        for b in range(BLOCKS):
+            nc.vector.tensor_tensor(slope_b[b][:], slope_b[b][:], rows_tb[:], ALU.add)
+        with_b = per_block("with_b", NEURONS)
+        for b in range(BLOCKS):
+            nc.vector.tensor_tensor(with_b[b][:], signals[b][:].indirect(list_b), slope_b[b][:], ALU.mult)
+        score = per_block("score", CLASSES)
+        for b in range(BLOCKS):
+            nc.vector.reduce_sum(score[b][:], with_b[b][:].rearrange("p (u r) -> p u r", r=GROUP), axis=AX.X)
+        for b in range(BLOCKS):
+            nc.vector.tensor_tensor(score[b][:], score[b][:], part[b][:], ALU.add)
+            nc.sync.dma_start(out[b * P : (b + 1) * P, :], score[b][:])

@@ -92,9 +92,8 @@ def tile_logicgatenetwork_kernel(tc, x, w, offs, out):
                 nc.scalar.copy(rows[:, first * P : (first + 2) * P], bank[:])
             return rows
 
-        rows_ta = as_rows(1, "ta")
         rows_tab = as_rows(3, "tab")
-        rows_tb = as_rows(2, "tb")
+        rows_ta = as_rows(1, "ta")
         t0_spread = held.tile([P, CHUNKS, P // GROUP], F32, name="t0_spread")
         nc.vector.tensor_tensor(
             t0_spread[:],
@@ -109,6 +108,23 @@ def tile_logicgatenetwork_kernel(tc, x, w, offs, out):
         def per_block(name, columns):
             return [held.tile([P, columns], F32, name=f"{name}{b}") for b in range(BLOCKS)]
 
+        curve = per_block("curve", NEURONS)
+        slope_bank = [psum.tile([P, NEURONS], F32, name=f"slope_bank{b}") for b in range(BLOCKS)]
+        slope_b = per_block("slope_b", NEURONS)
+        for b in range(BLOCKS):
+            for c in range(CHUNKS):
+                nc.tensor.matmul(
+                    slope_bank[b][:, c * P : (c + 1) * P],
+                    coef[:, 2, c : c + 1].to_broadcast([P, P]),
+                    ident[:],
+                    is_transpose=True,
+                    start=c == 0,
+                    stop=False,
+                )
+        for b in range(BLOCKS):
+            nc.vector.tensor_tensor(curve[b][:], signals[b][:].indirect(list_a), rows_tab[:], ALU.mult)
+            nc.tensor.matmul(slope_bank[b][:], ident[:], curve[b][:], start=False, stop=True)
+            nc.scalar.copy(slope_b[b][:], slope_bank[b][:])
         lin_a = per_block("lin_a", NEURONS)
         part = [psum.tile([P, CLASSES], F32, name=f"part{b}") for b in range(BLOCKS)]
         for b in range(BLOCKS):
@@ -117,11 +133,6 @@ def tile_logicgatenetwork_kernel(tc, x, w, offs, out):
             by_group = lin_a[b][:].rearrange("p (u r) -> p u r", r=GROUP)
             for r in range(GROUP):
                 nc.tensor.matmul(part[b][:], ident[:], by_group[:, :, r], start=False, stop=r == GROUP - 1)
-        slope_b = per_block("slope_b", NEURONS)
-        for b in range(BLOCKS):
-            nc.vector.tensor_tensor(slope_b[b][:], signals[b][:].indirect(list_a), rows_tab[:], ALU.mult)
-        for b in range(BLOCKS):
-            nc.vector.tensor_tensor(slope_b[b][:], slope_b[b][:], rows_tb[:], ALU.add)
         with_b = per_block("with_b", NEURONS)
         for b in range(BLOCKS):
             nc.vector.tensor_tensor(with_b[b][:], signals[b][:].indirect(list_b), slope_b[b][:], ALU.mult)

@@ -15,6 +15,7 @@ CLASSES = NEURONS // GROUP
 BLOCKS = SAMPLES // P
 CHUNKS = NEURONS // P
 LIST_COLS = NEURONS // 16
+PIECE = 256
 
 
 def tile_logicgatenetwork_kernel(tc, x, w, offs, out):
@@ -57,14 +58,11 @@ def tile_logicgatenetwork_kernel(tc, x, w, offs, out):
         logits_t = psum.tile([P, GATES * CHUNKS], F32, name="logits_t")
         nc.tensor.transpose(logits_t[:], logits[:], ident[: GATES * CHUNKS, : GATES * CHUNKS])
         by_neuron = logits_t[:].rearrange("p (q c) -> p c q", c=CHUNKS)
-        top = held.tile([P, CHUNKS], F32, name="top")
-        nc.vector.reduce_max(top[:], by_neuron, axis=AX.X)
-        shifted = held.tile([P, CHUNKS, GATES], F32, name="shifted")
-        nc.vector.tensor_tensor(
-            shifted[:], by_neuron, top[:].unsqueeze(2).to_broadcast([P, CHUNKS, GATES]), ALU.subtract
-        )
+        minus_top = held.tile([P, CHUNKS], F32, name="minus_top")
+        nc.vector.reduce_max(minus_top[:], by_neuron, axis=AX.X, negate=True)
         expw = held.tile([P, CHUNKS, GATES], F32, name="expw")
-        nc.scalar.activation(expw[:], shifted[:], ACT.Exp)
+        for c in range(CHUNKS):
+            nc.scalar.activation(expw[:, c, :], by_neuron[:, c, :], ACT.Exp, bias=minus_top[:, c : c + 1])
         weighted = held.tile([P, 4, CHUNKS, GATES], F32, name="weighted")
         nc.vector.tensor_tensor(
             weighted[:],
@@ -92,8 +90,9 @@ def tile_logicgatenetwork_kernel(tc, x, w, offs, out):
                 nc.scalar.copy(rows[:, first * P : (first + 2) * P], bank[:])
             return rows
 
-        rows_tab = as_rows(3, "tab")
         rows_ta = as_rows(1, "ta")
+        rows_tab = as_rows(3, "tab")
+        rows_tb = as_rows(2, "tb")
         t0_spread = held.tile([P, CHUNKS, P // GROUP], F32, name="t0_spread")
         nc.vector.tensor_tensor(
             t0_spread[:],
@@ -108,31 +107,25 @@ def tile_logicgatenetwork_kernel(tc, x, w, offs, out):
         def per_block(name, columns):
             return [held.tile([P, columns], F32, name=f"{name}{b}") for b in range(BLOCKS)]
 
-        curve = per_block("curve", NEURONS)
-        slope_bank = [psum.tile([P, NEURONS], F32, name=f"slope_bank{b}") for b in range(BLOCKS)]
-        slope_b = per_block("slope_b", NEURONS)
-        for b in range(BLOCKS):
-            for c in range(CHUNKS):
-                nc.tensor.matmul(
-                    slope_bank[b][:, c * P : (c + 1) * P],
-                    coef[:, 2, c : c + 1].to_broadcast([P, P]),
-                    ident[:],
-                    is_transpose=True,
-                    start=c == 0,
-                    stop=False,
-                )
-        for b in range(BLOCKS):
-            nc.vector.tensor_tensor(curve[b][:], signals[b][:].indirect(list_a), rows_tab[:], ALU.mult)
-            nc.tensor.matmul(slope_bank[b][:], ident[:], curve[b][:], start=False, stop=True)
-            nc.scalar.copy(slope_b[b][:], slope_bank[b][:])
         lin_a = per_block("lin_a", NEURONS)
         part = [psum.tile([P, CLASSES], F32, name=f"part{b}") for b in range(BLOCKS)]
         for b in range(BLOCKS):
-            nc.vector.tensor_tensor(lin_a[b][:], signals[b][:].indirect(list_a), rows_ta[:], ALU.mult)
+            for first in range(0, NEURONS, PIECE):
+                nc.vector.tensor_tensor(
+                    lin_a[b][:, first : first + PIECE],
+                    signals[b][:].indirect(offsets[:, first // 16 : (first + PIECE) // 16]),
+                    rows_ta[:, first : first + PIECE],
+                    ALU.mult,
+                )
             nc.tensor.matmul(part[b][:], ones[:], t0_spread[:].rearrange("p c v -> p (c v)"), start=True, stop=False)
             by_group = lin_a[b][:].rearrange("p (u r) -> p u r", r=GROUP)
             for r in range(GROUP):
                 nc.tensor.matmul(part[b][:], ident[:], by_group[:, :, r], start=False, stop=r == GROUP - 1)
+        slope_b = per_block("slope_b", NEURONS)
+        for b in range(BLOCKS):
+            nc.vector.tensor_tensor(slope_b[b][:], signals[b][:].indirect(list_a), rows_tab[:], ALU.mult)
+        for b in range(BLOCKS):
+            nc.vector.tensor_tensor(slope_b[b][:], slope_b[b][:], rows_tb[:], ALU.add)
         with_b = per_block("with_b", NEURONS)
         for b in range(BLOCKS):
             nc.vector.tensor_tensor(with_b[b][:], signals[b][:].indirect(list_b), slope_b[b][:], ALU.mult)

@@ -14,8 +14,10 @@ GROUP = 4
 CLASSES = NEURONS // GROUP
 BLOCKS = SAMPLES // P
 CHUNKS = NEURONS // P
+CHUNK_CLASSES = P // GROUP
 LIST_COLS = NEURONS // 16
 PIECE = 256
+T0, TB, TA, TAB = 0, 1, 2, 3
 
 
 def tile_logicgatenetwork_kernel(tc, x, w, offs, out):
@@ -40,7 +42,7 @@ def tile_logicgatenetwork_kernel(tc, x, w, offs, out):
         make_identity(nc, ident[:])
         ones = held.tile([P, P], F32, name="ones")
         nc.vector.memset(ones[:], 1.0)
-        group_of = held.tile([P, P // GROUP], F32, name="group_of")
+        group_of = held.tile([P, CHUNK_CLASSES], F32, name="group_of")
         nc.vector.reduce_sum(group_of[:], ident[:].rearrange("p (v r) -> p v r", r=GROUP), axis=AX.X)
         truth = held.tile([P, 4, GATES], F32, name="truth")
         nc.vector.memset(truth[:], 0.0)
@@ -49,11 +51,11 @@ def tile_logicgatenetwork_kernel(tc, x, w, offs, out):
             upper_half = truth[:, i, :].rearrange("p (n s) -> p n s", s=period)[:, :, period // 2 :]
             nc.vector.memset(upper_half, 1.0)
         gate_poly = held.tile([P, 4, GATES], F32, name="gate_poly")
-        nc.vector.tensor_copy(gate_poly[:, 0, :], truth[:, 0, :])
-        nc.vector.tensor_sub(gate_poly[:, 1, :], truth[:, 2, :], truth[:, 0, :])
-        nc.vector.tensor_sub(gate_poly[:, 2, :], truth[:, 1, :], truth[:, 0, :])
-        nc.vector.tensor_sub(gate_poly[:, 3, :], truth[:, 3, :], truth[:, 2, :])
-        nc.vector.tensor_sub(gate_poly[:, 3, :], gate_poly[:, 3, :], gate_poly[:, 2, :])
+        nc.vector.tensor_copy(gate_poly[:, T0, :], truth[:, 0, :])
+        nc.vector.tensor_sub(gate_poly[:, TB, :], truth[:, 1, :], truth[:, 0, :])
+        nc.vector.tensor_sub(gate_poly[:, TA, :], truth[:, 2, :], truth[:, 0, :])
+        nc.vector.tensor_sub(gate_poly[:, TAB, :], truth[:, 3, :], truth[:, 2, :])
+        nc.vector.tensor_sub(gate_poly[:, TAB, :], gate_poly[:, TAB, :], gate_poly[:, TB, :])
 
         logits_t = psum.tile([P, GATES * CHUNKS], F32, name="logits_t")
         nc.tensor.transpose(logits_t[:], logits[:], ident[: GATES * CHUNKS, : GATES * CHUNKS])
@@ -61,8 +63,31 @@ def tile_logicgatenetwork_kernel(tc, x, w, offs, out):
         minus_top = held.tile([P, CHUNKS], F32, name="minus_top")
         nc.vector.reduce_max(minus_top[:], by_neuron, axis=AX.X, negate=True)
         expw = held.tile([P, CHUNKS, GATES], F32, name="expw")
+        denom = held.tile([P, CHUNKS], F32, name="denom")
         for c in range(CHUNKS):
-            nc.scalar.activation(expw[:, c, :], by_neuron[:, c, :], ACT.Exp, bias=minus_top[:, c : c + 1])
+            nc.scalar.activation(
+                expw[:, c, :],
+                by_neuron[:, c, :],
+                ACT.Exp,
+                bias=minus_top[:, c : c + 1],
+                accum_out=denom[:, c : c + 1],
+            )
+        inv = held.tile([P, CHUNKS], F32, name="inv")
+        nc.vector.reciprocal(inv[:], denom[:])
+
+        def as_rows(by_chunk, name):
+            rows = held.tile([P, NEURONS], F32, name="rows_" + name)
+            for first in range(0, CHUNKS, 2):
+                bank = row_banks.tile([P, 2 * P], F32, name="bank")
+                for i in range(2):
+                    nc.tensor.transpose(
+                        bank[:, i * P : (i + 1) * P], by_chunk[:, first + i : first + i + 1].to_broadcast([P, P]), ident[:]
+                    )
+                nc.scalar.copy(rows[:, first * P : (first + 2) * P], bank[:])
+            return rows
+
+        rows_inv = as_rows(inv[:], "inv")
+
         weighted = held.tile([P, 4, CHUNKS, GATES], F32, name="weighted")
         nc.vector.tensor_tensor(
             weighted[:],
@@ -70,60 +95,58 @@ def tile_logicgatenetwork_kernel(tc, x, w, offs, out):
             gate_poly[:].unsqueeze(2).to_broadcast([P, 4, CHUNKS, GATES]),
             ALU.mult,
         )
-        denom = held.tile([P, CHUNKS], F32, name="denom")
-        nc.vector.reduce_sum(denom[:], expw[:], axis=AX.X)
-        sums = held.tile([P, 4, CHUNKS], F32, name="sums")
-        nc.vector.reduce_sum(sums[:], weighted[:], axis=AX.X)
-        inv = held.tile([P, CHUNKS], F32, name="inv")
-        nc.vector.reciprocal(inv[:], denom[:])
         coef = held.tile([P, 4, CHUNKS], F32, name="coef")
-        nc.vector.tensor_tensor(coef[:], sums[:], inv[:].unsqueeze(1).to_broadcast([P, 4, CHUNKS]), ALU.mult)
-
-        def as_rows(k, name):
-            rows = held.tile([P, NEURONS], F32, name="rows_" + name)
-            for first in range(0, CHUNKS, 2):
-                bank = row_banks.tile([P, 2 * P], F32, name="bank")
-                for i in range(2):
-                    nc.tensor.transpose(
-                        bank[:, i * P : (i + 1) * P], coef[:, k, first + i : first + i + 1].to_broadcast([P, P]), ident[:]
-                    )
-                nc.scalar.copy(rows[:, first * P : (first + 2) * P], bank[:])
-            return rows
-
-        rows_ta = as_rows(1, "ta")
-        rows_tab = as_rows(3, "tab")
-        rows_tb = as_rows(2, "tb")
-        t0_spread = held.tile([P, CHUNKS, P // GROUP], F32, name="t0_spread")
+        nc.vector.reduce_sum(coef[:], weighted[:], axis=AX.X)
+        rows_tab = as_rows(coef[:, TAB, :], "tab")
+        whole = held.tile([P, 2, CHUNKS], F32, name="whole")
         nc.vector.tensor_tensor(
-            t0_spread[:],
-            group_of[:].unsqueeze(1).to_broadcast([P, CHUNKS, P // GROUP]),
-            coef[:, 0, :].unsqueeze(2).to_broadcast([P, CHUNKS, P // GROUP]),
-            ALU.mult,
+            whole[:], coef[:, T0 : TB + 1, :], inv[:].unsqueeze(1).to_broadcast([P, 2, CHUNKS]), ALU.mult
         )
-
-        list_a = offsets[:, 0:LIST_COLS]
-        list_b = offsets[:, LIST_COLS : 2 * LIST_COLS]
+        rows_tb = as_rows(whole[:, TB, :], "tb")
 
         def per_block(name, columns):
             return [held.tile([P, columns], F32, name=f"{name}{b}") for b in range(BLOCKS)]
 
-        lin_a = per_block("lin_a", NEURONS)
-        part = [psum.tile([P, CLASSES], F32, name=f"part{b}") for b in range(BLOCKS)]
+        a_scaled = per_block("a_scaled", NEURONS)
         for b in range(BLOCKS):
             for first in range(0, NEURONS, PIECE):
                 nc.vector.tensor_tensor(
-                    lin_a[b][:, first : first + PIECE],
+                    a_scaled[b][:, first : first + PIECE],
                     signals[b][:].indirect(offsets[:, first // 16 : (first + PIECE) // 16]),
-                    rows_ta[:, first : first + PIECE],
+                    rows_inv[:, first : first + PIECE],
                     ALU.mult,
                 )
+
+        t0_spread = held.tile([P, CHUNKS, CHUNK_CLASSES], F32, name="t0_spread")
+        ta_spread = held.tile([P, CHUNKS, CHUNK_CLASSES], F32, name="ta_spread")
+        for spread, numbers in ((t0_spread, whole[:, T0, :]), (ta_spread, coef[:, TA, :])):
+            nc.vector.tensor_tensor(
+                spread[:],
+                group_of[:].unsqueeze(1).to_broadcast([P, CHUNKS, CHUNK_CLASSES]),
+                numbers.unsqueeze(2).to_broadcast([P, CHUNKS, CHUNK_CLASSES]),
+                ALU.mult,
+            )
+        part = [psum.tile([P, CLASSES], F32, name=f"part{b}") for b in range(BLOCKS)]
+        for b in range(BLOCKS):
+            turned_bank = psum.tile([P, NEURONS], F32, name=f"turned_bank{b}")
+            for c in range(CHUNKS):
+                nc.tensor.transpose(turned_bank[:, c * P : (c + 1) * P], a_scaled[b][:, c * P : (c + 1) * P], ident[:])
+            turned = held.tile([P, NEURONS], F32, name=f"turned{b}")
+            nc.scalar.copy(turned[:], turned_bank[:])
             nc.tensor.matmul(part[b][:], ones[:], t0_spread[:].rearrange("p c v -> p (c v)"), start=True, stop=False)
-            by_group = lin_a[b][:].rearrange("p (u r) -> p u r", r=GROUP)
-            for r in range(GROUP):
-                nc.tensor.matmul(part[b][:], ident[:], by_group[:, :, r], start=False, stop=r == GROUP - 1)
+            for c in range(CHUNKS):
+                nc.tensor.matmul(
+                    part[b][:, c * CHUNK_CLASSES : (c + 1) * CHUNK_CLASSES],
+                    turned[:, c * P : (c + 1) * P],
+                    ta_spread[:, c, :],
+                    start=False,
+                    stop=c == CHUNKS - 1,
+                )
+
+        list_b = offsets[:, LIST_COLS : 2 * LIST_COLS]
         slope_b = per_block("slope_b", NEURONS)
         for b in range(BLOCKS):
-            nc.vector.tensor_tensor(slope_b[b][:], signals[b][:].indirect(list_a), rows_tab[:], ALU.mult)
+            nc.vector.tensor_tensor(slope_b[b][:], a_scaled[b][:], rows_tab[:], ALU.mult)
         for b in range(BLOCKS):
             nc.vector.tensor_tensor(slope_b[b][:], slope_b[b][:], rows_tb[:], ALU.add)
         with_b = per_block("with_b", NEURONS)

@@ -40,8 +40,6 @@ def tile_logicgatenetwork_kernel(tc, x, w, offs, out):
 
         ident = held.tile([P, P], F32, name="ident")
         make_identity(nc, ident[:])
-        ones = held.tile([P, P], F32, name="ones")
-        nc.vector.memset(ones[:], 1.0)
         group_of = held.tile([P, CHUNK_CLASSES], F32, name="group_of")
         nc.vector.reduce_sum(group_of[:], ident[:].rearrange("p (v r) -> p v r", r=GROUP), axis=AX.X)
         truth = held.tile([P, 4, GATES], F32, name="truth")
@@ -117,30 +115,28 @@ def tile_logicgatenetwork_kernel(tc, x, w, offs, out):
                     ALU.mult,
                 )
 
-        t0_spread = held.tile([P, CHUNKS, CHUNK_CLASSES], F32, name="t0_spread")
-        ta_spread = held.tile([P, CHUNKS, CHUNK_CLASSES], F32, name="ta_spread")
-        for spread, numbers in ((t0_spread, whole[:, T0, :]), (ta_spread, coef[:, TA, :])):
-            nc.vector.tensor_tensor(
-                spread[:],
-                group_of[:].unsqueeze(1).to_broadcast([P, CHUNKS, CHUNK_CLASSES]),
-                numbers.unsqueeze(2).to_broadcast([P, CHUNKS, CHUNK_CLASSES]),
-                ALU.mult,
-            )
         part = [psum.tile([P, CLASSES], F32, name=f"part{b}") for b in range(BLOCKS)]
+        chunks = [slice(c * P, (c + 1) * P) for c in range(CHUNKS)]
         for b in range(BLOCKS):
             turned_bank = psum.tile([P, NEURONS], F32, name=f"turned_bank{b}")
+            linear = held.tile([P, NEURONS], F32, name=f"linear{b}")
             for c in range(CHUNKS):
-                nc.tensor.transpose(turned_bank[:, c * P : (c + 1) * P], a_scaled[b][:, c * P : (c + 1) * P], ident[:])
-            turned = held.tile([P, NEURONS], F32, name=f"turned{b}")
-            nc.scalar.copy(turned[:], turned_bank[:])
-            nc.tensor.matmul(part[b][:], ones[:], t0_spread[:].rearrange("p c v -> p (c v)"), start=True, stop=False)
+                nc.tensor.transpose(turned_bank[:, chunks[c]], a_scaled[b][:, chunks[c]], ident[:])
+            for c in range(CHUNKS):
+                nc.scalar.activation(
+                    linear[:, chunks[c]],
+                    turned_bank[:, chunks[c]],
+                    ACT.Identity,
+                    scale=coef[:, TA, c : c + 1],
+                    bias=whole[:, T0, c : c + 1],
+                )
             for c in range(CHUNKS):
                 nc.tensor.matmul(
                     part[b][:, c * CHUNK_CLASSES : (c + 1) * CHUNK_CLASSES],
-                    turned[:, c * P : (c + 1) * P],
-                    ta_spread[:, c, :],
-                    start=False,
-                    stop=c == CHUNKS - 1,
+                    linear[:, chunks[c]],
+                    group_of[:],
+                    start=True,
+                    stop=True,
                 )
 
         list_b = offsets[:, LIST_COLS : 2 * LIST_COLS]

@@ -71,12 +71,13 @@ def tile_logicgatenetwork_kernel(tc, x, w, offs, out):
                 accum_out=denom[:, c : c + 1],
             )
         inv = held.tile([P, CHUNKS], F32, name="inv")
-        nc.vector.reciprocal(inv[:], denom[:])
+        for first in range(0, CHUNKS, 2):
+            nc.vector.reciprocal(inv[:, first : first + 2], denom[:, first : first + 2])
 
         def as_rows(by_chunk, name):
             rows = held.tile([P, NEURONS], F32, name="rows_" + name)
             for first in range(0, CHUNKS, 2):
-                bank = row_banks.tile([P, 2 * P], F32, name="bank")
+                bank = row_banks.tile([P, PIECE], F32, name="bank")
                 for i in range(2):
                     nc.tensor.transpose(
                         bank[:, i * P : (i + 1) * P], by_chunk[:, first + i : first + i + 1].to_broadcast([P, P]), ident[:]
@@ -106,8 +107,8 @@ def tile_logicgatenetwork_kernel(tc, x, w, offs, out):
             return [held.tile([P, columns], F32, name=f"{name}{b}") for b in range(BLOCKS)]
 
         a_scaled = per_block("a_scaled", NEURONS)
-        for b in range(BLOCKS):
-            for first in range(0, NEURONS, PIECE):
+        for first in range(0, NEURONS, PIECE):
+            for b in range(BLOCKS):
                 nc.vector.tensor_tensor(
                     a_scaled[b][:, first : first + PIECE],
                     signals[b][:].indirect(offsets[:, first // 16 : (first + PIECE) // 16]),

@@ -107,12 +107,12 @@ def tile_logicgatenetwork_kernel(tc, x, w, offs, out):
             return [held.tile([P, columns], F32, name=f"{name}{b}") for b in range(BLOCKS)]
 
         a_scaled = per_block("a_scaled", NEURONS)
-        for first in range(0, NEURONS, PIECE):
-            for b in range(BLOCKS):
+        for b, piece in ((0, PIECE), (1, NEURONS)):
+            for first in range(0, NEURONS, piece):
                 nc.vector.tensor_tensor(
-                    a_scaled[b][:, first : first + PIECE],
-                    signals[b][:].indirect(offsets[:, first // 16 : (first + PIECE) // 16]),
-                    rows_inv[:, first : first + PIECE],
+                    a_scaled[b][:, first : first + piece],
+                    signals[b][:].indirect(offsets[:, first // 16 : (first + piece) // 16]),
+                    rows_inv[:, first : first + piece],
                     ALU.mult,
                 )
 

@@ -40,6 +40,10 @@ def tile_logicgatenetwork_kernel(tc, x, w, offs, out):
 
         ident = held.tile([P, P], F32, name="ident")
         make_identity(nc, ident[:])
+        gates_together = held.tile([GATES * CHUNKS, CHUNKS, GATES], F32, name="gates_together")
+        nc.vector.tensor_copy(
+            gates_together[:], ident[: GATES * CHUNKS, : GATES * CHUNKS].rearrange("p (q c) -> p c q", c=CHUNKS)
+        )
         group_of = held.tile([P, CHUNK_CLASSES], F32, name="group_of")
         nc.vector.reduce_sum(group_of[:], ident[:].rearrange("p (v r) -> p v r", r=GROUP), axis=AX.X)
         truth = held.tile([P, 4, GATES], F32, name="truth")
@@ -56,8 +60,8 @@ def tile_logicgatenetwork_kernel(tc, x, w, offs, out):
         nc.vector.tensor_sub(gate_poly[:, TAB, :], gate_poly[:, TAB, :], gate_poly[:, TB, :])
 
         logits_t = psum.tile([P, GATES * CHUNKS], F32, name="logits_t")
-        nc.tensor.transpose(logits_t[:], logits[:], ident[: GATES * CHUNKS, : GATES * CHUNKS])
-        by_neuron = logits_t[:].rearrange("p (q c) -> p c q", c=CHUNKS)
+        nc.tensor.transpose(logits_t[:], logits[:], gates_together[:].rearrange("p c q -> p (c q)"))
+        by_neuron = logits_t[:].rearrange("p (c q) -> p c q", c=CHUNKS)
         minus_top = held.tile([P, CHUNKS], F32, name="minus_top")
         nc.vector.reduce_max(minus_top[:], by_neuron, axis=AX.X, negate=True)
         expw = held.tile([P, CHUNKS, GATES], F32, name="expw")

@@ -24,8 +24,9 @@ def tile_logicgatenetwork_kernel(tc, x, w, offs, out):
     nc = tc.nc
     with (
         tc.tile_pool(name="held", bufs=1) as held,
-        tc.psum_pool(name="psum", bufs=1) as psum,
-        tc.psum_pool(name="row_banks", bufs=3) as row_banks,
+        tc.psum_pool(name="row_banks", bufs=4) as row_banks,
+        tc.psum_pool(name="turned_banks", bufs=2) as turned_banks,
+        tc.psum_pool(name="first_and_last", bufs=2) as first_and_last,
     ):
         logits = held.tile([GATES * CHUNKS, P], F32, name="logits")
         nc.sync.dma_start(logits[:], w.rearrange("q (c n) -> (q c) n", c=CHUNKS))
@@ -46,22 +47,10 @@ def tile_logicgatenetwork_kernel(tc, x, w, offs, out):
         )
         group_of = held.tile([P, CHUNK_CLASSES], F32, name="group_of")
         nc.vector.reduce_sum(group_of[:], ident[:].rearrange("p (v r) -> p v r", r=GROUP), axis=AX.X)
-        truth = held.tile([P, 4, GATES], F32, name="truth")
-        nc.vector.memset(truth[:], 0.0)
-        for i in range(4):
-            period = GATES >> i
-            upper_half = truth[:, i, :].rearrange("p (n s) -> p n s", s=period)[:, :, period // 2 :]
-            nc.vector.memset(upper_half, 1.0)
-        gate_poly = held.tile([P, 4, GATES], F32, name="gate_poly")
-        nc.vector.tensor_copy(gate_poly[:, T0, :], truth[:, 0, :])
-        nc.vector.tensor_sub(gate_poly[:, TB, :], truth[:, 1, :], truth[:, 0, :])
-        nc.vector.tensor_sub(gate_poly[:, TA, :], truth[:, 2, :], truth[:, 0, :])
-        nc.vector.tensor_sub(gate_poly[:, TAB, :], truth[:, 3, :], truth[:, 2, :])
-        nc.vector.tensor_sub(gate_poly[:, TAB, :], gate_poly[:, TAB, :], gate_poly[:, TB, :])
 
-        logits_t = psum.tile([P, GATES * CHUNKS], F32, name="logits_t")
-        nc.tensor.transpose(logits_t[:], logits[:], gates_together[:].rearrange("p c q -> p (c q)"))
-        by_neuron = logits_t[:].rearrange("p (c q) -> p c q", c=CHUNKS)
+        logits_t = first_and_last.tile([P, CLASSES], F32, name="bank")[:, : GATES * CHUNKS]
+        nc.tensor.transpose(logits_t, logits[:], gates_together[:].rearrange("p c q -> p (c q)"))
+        by_neuron = logits_t.rearrange("p (c q) -> p c q", c=CHUNKS)
         minus_top = held.tile([P, CHUNKS], F32, name="minus_top")
         nc.vector.reduce_max(minus_top[:], by_neuron, axis=AX.X, negate=True)
         expw = held.tile([P, CHUNKS, GATES], F32, name="expw")
@@ -74,38 +63,48 @@ def tile_logicgatenetwork_kernel(tc, x, w, offs, out):
                 bias=minus_top[:, c : c + 1],
                 accum_out=denom[:, c : c + 1],
             )
-        inv = held.tile([P, CHUNKS], F32, name="inv")
+
+        chunks = [slice(c * P, (c + 1) * P) for c in range(CHUNKS)]
+
+        def in_halves(n):
+            return [slice(0, n // 2), slice(n // 2, n)]
+
+        halves, half_lists, half_classes = in_halves(NEURONS), in_halves(LIST_COLS), in_halves(CLASSES)
+
+        def turn_into_row(bank_columns, column):
+            nc.tensor.transpose(bank_columns, column.to_broadcast([P, P]), ident[:])
+
+        rows_denom = held.tile([P, NEURONS], F32, name="rows_denom")
         for first in range(0, CHUNKS, 2):
-            nc.vector.reciprocal(inv[:, first : first + 2], denom[:, first : first + 2])
+            bank = row_banks.tile([P, NEURONS], F32, name="bank")
+            for i in range(2):
+                turn_into_row(bank[:, chunks[i]], denom[:, first + i : first + i + 1])
+            nc.scalar.copy(rows_denom[:, first * P : (first + 2) * P], bank[:, :PIECE])
 
-        def as_rows(by_chunk, name):
-            rows = held.tile([P, NEURONS], F32, name="rows_" + name)
-            for first in range(0, CHUNKS, 2):
-                bank = row_banks.tile([P, PIECE], F32, name="bank")
-                for i in range(2):
-                    nc.tensor.transpose(
-                        bank[:, i * P : (i + 1) * P], by_chunk[:, first + i : first + i + 1].to_broadcast([P, P]), ident[:]
-                    )
-                nc.scalar.copy(rows[:, first * P : (first + 2) * P], bank[:])
-            return rows
-
-        rows_inv = as_rows(inv[:], "inv")
-
-        weighted = held.tile([P, 4, CHUNKS, GATES], F32, name="weighted")
+        numer = held.tile([P, 4, CHUNKS], F32, name="numer")
+        for i in range(4):
+            stretch = GATES >> i
+            bit_set = expw[:].rearrange("p c (n s) -> p c n s", s=stretch)[:, :, :, stretch // 2 :]
+            nc.vector.reduce_sum(numer[:, i, :], bit_set, axis=AX.XY)
+        inv = held.tile([P, 2, CHUNKS], F32, name="inv")
+        nc.vector.reciprocal(inv[:, 0, :], denom[:])
+        by_ab = numer[:].rearrange("p (i j) c -> p i j c", i=2)
+        nc.vector.tensor_sub(by_ab[:, :, 1, :], by_ab[:, :, 1, :], by_ab[:, :, 0, :])
+        nc.vector.tensor_mul(inv[:, 1, :], inv[:, 0, :], inv[:, 0, :])
+        nc.vector.tensor_sub(by_ab[:, 1, :, :], by_ab[:, 1, :, :], by_ab[:, 0, :, :])
+        coef = held.tile([P, 4, CHUNKS], F32, name="coef")
         nc.vector.tensor_tensor(
-            weighted[:],
-            expw[:].unsqueeze(1).to_broadcast([P, 4, CHUNKS, GATES]),
-            gate_poly[:].unsqueeze(2).to_broadcast([P, 4, CHUNKS, GATES]),
+            coef[:].rearrange("p (i j) c -> p i j c", i=2),
+            by_ab,
+            inv[:].unsqueeze(2).to_broadcast([P, 2, 2, CHUNKS]),
             ALU.mult,
         )
-        coef = held.tile([P, 4, CHUNKS], F32, name="coef")
-        nc.vector.reduce_sum(coef[:], weighted[:], axis=AX.X)
-        rows_tab = as_rows(coef[:, TAB, :], "tab")
-        whole = held.tile([P, 2, CHUNKS], F32, name="whole")
-        nc.vector.tensor_tensor(
-            whole[:], coef[:, T0 : TB + 1, :], inv[:].unsqueeze(1).to_broadcast([P, 2, CHUNKS]), ALU.mult
-        )
-        rows_tb = as_rows(whole[:, TB, :], "tb")
+
+        rows_tab = row_banks.tile([P, NEURONS], F32, name="bank")
+        rows_tb = row_banks.tile([P, NEURONS], F32, name="bank")
+        for rows, k in ((rows_tab, TAB), (rows_tb, TB)):
+            for c in range(CHUNKS):
+                turn_into_row(rows[:, chunks[c]], coef[:, k, c : c + 1])
 
         def per_block(name, columns):
             return [held.tile([P, columns], F32, name=f"{name}{b}") for b in range(BLOCKS)]
@@ -116,46 +115,54 @@ def tile_logicgatenetwork_kernel(tc, x, w, offs, out):
                 nc.vector.tensor_tensor(
                     a_scaled[b][:, first : first + piece],
                     signals[b][:].indirect(offsets[:, first // 16 : (first + piece) // 16]),
-                    rows_inv[:, first : first + piece],
+                    rows_denom[:, first : first + piece],
                     ALU.mult,
                 )
 
-        part = [psum.tile([P, CLASSES], F32, name=f"part{b}") for b in range(BLOCKS)]
-        chunks = [slice(c * P, (c + 1) * P) for c in range(CHUNKS)]
+        part = []
         for b in range(BLOCKS):
-            turned_bank = psum.tile([P, NEURONS], F32, name=f"turned_bank{b}")
+            turned = turned_banks.tile([P, NEURONS], F32, name="bank")
             linear = held.tile([P, NEURONS], F32, name=f"linear{b}")
             for c in range(CHUNKS):
-                nc.tensor.transpose(turned_bank[:, chunks[c]], a_scaled[b][:, chunks[c]], ident[:])
+                nc.tensor.transpose(turned[:, chunks[c]], a_scaled[b][:, chunks[c]], ident[:])
             for c in range(CHUNKS):
                 nc.scalar.activation(
                     linear[:, chunks[c]],
-                    turned_bank[:, chunks[c]],
+                    turned[:, chunks[c]],
                     ACT.Identity,
                     scale=coef[:, TA, c : c + 1],
-                    bias=whole[:, T0, c : c + 1],
+                    bias=coef[:, T0, c : c + 1],
                 )
+            part.append(first_and_last.tile([P, CLASSES], F32, name="bank"))
             for c in range(CHUNKS):
                 nc.tensor.matmul(
                     part[b][:, c * CHUNK_CLASSES : (c + 1) * CHUNK_CLASSES],
                     linear[:, chunks[c]],
                     group_of[:],
-                    start=True,
-                    stop=True,
+                    start=c == 0,
+                    stop=b == 1 and c == CHUNKS - 1,
                 )
 
-        list_b = offsets[:, LIST_COLS : 2 * LIST_COLS]
+        list_b = offsets[:, LIST_COLS:]
         slope_b = per_block("slope_b", NEURONS)
         for b in range(BLOCKS):
             nc.vector.tensor_tensor(slope_b[b][:], a_scaled[b][:], rows_tab[:], ALU.mult)
         for b in range(BLOCKS):
             nc.vector.tensor_tensor(slope_b[b][:], slope_b[b][:], rows_tb[:], ALU.add)
         with_b = per_block("with_b", NEURONS)
-        for b in range(BLOCKS):
-            nc.vector.tensor_tensor(with_b[b][:], signals[b][:].indirect(list_b), slope_b[b][:], ALU.mult)
         score = per_block("score", CLASSES)
-        for b in range(BLOCKS):
-            nc.vector.reduce_sum(score[b][:], with_b[b][:].rearrange("p (u r) -> p u r", r=GROUP), axis=AX.X)
-        for b in range(BLOCKS):
-            nc.vector.tensor_tensor(score[b][:], score[b][:], part[b][:], ALU.add)
-            nc.sync.dma_start(out[b * P : (b + 1) * P, :], score[b][:])
+        by_class = [with_b[b][:].rearrange("p (u r) -> p u r", r=GROUP) for b in range(BLOCKS)]
+        nc.vector.tensor_tensor(with_b[0][:], signals[0][:].indirect(list_b), slope_b[0][:], ALU.mult)
+        for half, half_list in zip(halves, half_lists):
+            nc.vector.tensor_tensor(
+                with_b[1][:, half], signals[1][:].indirect(list_b[:, half_list]), slope_b[1][:, half], ALU.mult
+            )
+        for r in range(GROUP):
+            nc.tensor.matmul(part[0][:], ident[:], by_class[0][:, :, r], start=False, stop=r == GROUP - 1)
+        nc.scalar.copy(score[0][:], part[0][:])
+        nc.sync.dma_start(out[:P, :], score[0][:])
+        for half in half_classes:
+            nc.vector.reduce_sum(score[1][:, half], by_class[1][:, half, :], axis=AX.X)
+        for half in half_classes:
+            nc.vector.tensor_tensor(score[1][:, half], score[1][:, half], part[1][:, half], ALU.add)
+        nc.sync.dma_start(out[P : 2 * P, :], score[1][:])

@@ -66,11 +66,6 @@ def tile_logicgatenetwork_kernel(tc, x, w, offs, out):
 
         chunks = [slice(c * P, (c + 1) * P) for c in range(CHUNKS)]
 
-        def in_halves(n):
-            return [slice(0, n // 2), slice(n // 2, n)]
-
-        halves, half_lists, half_classes = in_halves(NEURONS), in_halves(LIST_COLS), in_halves(CLASSES)
-
         def turn_into_row(bank_columns, column):
             nc.tensor.transpose(bank_columns, column.to_broadcast([P, P]), ident[:])
 
@@ -139,8 +134,8 @@ def tile_logicgatenetwork_kernel(tc, x, w, offs, out):
                     part[b][:, c * CHUNK_CLASSES : (c + 1) * CHUNK_CLASSES],
                     linear[:, chunks[c]],
                     group_of[:],
-                    start=c == 0,
-                    stop=b == 1 and c == CHUNKS - 1,
+                    start=True,
+                    stop=True,
                 )
 
         list_b = offsets[:, LIST_COLS:]
@@ -151,18 +146,10 @@ def tile_logicgatenetwork_kernel(tc, x, w, offs, out):
             nc.vector.tensor_tensor(slope_b[b][:], slope_b[b][:], rows_tb[:], ALU.add)
         with_b = per_block("with_b", NEURONS)
         score = per_block("score", CLASSES)
-        by_class = [with_b[b][:].rearrange("p (u r) -> p u r", r=GROUP) for b in range(BLOCKS)]
-        nc.vector.tensor_tensor(with_b[0][:], signals[0][:].indirect(list_b), slope_b[0][:], ALU.mult)
-        for half, half_list in zip(halves, half_lists):
-            nc.vector.tensor_tensor(
-                with_b[1][:, half], signals[1][:].indirect(list_b[:, half_list]), slope_b[1][:, half], ALU.mult
-            )
-        for r in range(GROUP):
-            nc.tensor.matmul(part[0][:], ident[:], by_class[0][:, :, r], start=False, stop=r == GROUP - 1)
-        nc.scalar.copy(score[0][:], part[0][:])
-        nc.sync.dma_start(out[:P, :], score[0][:])
-        for half in half_classes:
-            nc.vector.reduce_sum(score[1][:, half], by_class[1][:, half, :], axis=AX.X)
-        for half in half_classes:
-            nc.vector.tensor_tensor(score[1][:, half], score[1][:, half], part[1][:, half], ALU.add)
-        nc.sync.dma_start(out[P : 2 * P, :], score[1][:])
+        for b in range(BLOCKS):
+            nc.vector.tensor_tensor(with_b[b][:], signals[b][:].indirect(list_b), slope_b[b][:], ALU.mult)
+        for b in range(BLOCKS):
+            nc.vector.reduce_sum(score[b][:], with_b[b][:].rearrange("p (u r) -> p u r", r=GROUP), axis=AX.X)
+        for b in range(BLOCKS):
+            nc.vector.tensor_tensor(score[b][:], score[b][:], part[b][:], ALU.add)
+            nc.sync.dma_start(out[b * P : (b + 1) * P, :], score[b][:])

@@ -76,25 +76,29 @@ def tile_logicgatenetwork_kernel(tc, x, w, offs, out):
                 turn_into_row(bank[:, chunks[i]], denom[:, first + i : first + i + 1])
             nc.scalar.copy(rows_denom[:, first * P : (first + 2) * P], bank[:, :PIECE])
 
+        diff = held.tile([P, CHUNKS, 3, 4], F32, name="diff")
+        by_four = expw[:].rearrange("p c (m r) -> p c m r", r=4)
+        nc.vector.tensor_sub(diff[:, :, 0, :], by_four[:, :, :, 1], by_four[:, :, :, 2])
+        nc.vector.tensor_sub(diff[:, :, 1, :], by_four[:, :, 2, :], by_four[:, :, 1, :])
+        by_bit = expw[:].rearrange("p c (i j k l) -> p c i j k l", i=2, j=2, k=2)
+        nc.vector.tensor_sub(
+            diff[:, :, 2, :].rearrange("p c (j l) -> p c j l", j=2), by_bit[:, :, 0, :, 1, :], by_bit[:, :, 1, :, 0, :]
+        )
         numer = held.tile([P, 4, CHUNKS], F32, name="numer")
-        for i in range(4):
-            stretch = GATES >> i
-            bit_set = expw[:].rearrange("p c (n s) -> p c n s", s=stretch)[:, :, :, stretch // 2 :]
-            nc.vector.reduce_sum(numer[:, i, :], bit_set, axis=AX.XY)
+        nc.vector.reduce_sum(numer[:, T0, :], expw[:, :, 8:], axis=AX.X)
         inv = held.tile([P, 2, CHUNKS], F32, name="inv")
         nc.vector.reciprocal(inv[:, 0, :], denom[:])
-        by_ab = numer[:].rearrange("p (i j) c -> p i j c", i=2)
-        nc.vector.tensor_sub(by_ab[:, :, 1, :], by_ab[:, :, 1, :], by_ab[:, :, 0, :])
+        nc.vector.reduce_sum(numer[:, TAB, :], diff[:, :, 0:2, :], axis=AX.XY)
+        nc.vector.reduce_sum(numer[:, TB, :], diff[:, :, 1, :], axis=AX.X, negate=True)
+        nc.vector.reduce_sum(numer[:, TA, :], diff[:, :, 2, :], axis=AX.X)
         nc.vector.tensor_mul(inv[:, 1, :], inv[:, 0, :], inv[:, 0, :])
-        nc.vector.tensor_sub(by_ab[:, 1, :, :], by_ab[:, 1, :, :], by_ab[:, 0, :, :])
         coef = held.tile([P, 4, CHUNKS], F32, name="coef")
         nc.vector.tensor_tensor(
-            coef[:].rearrange("p (i j) c -> p i j c", i=2),
-            by_ab,
+            coef[:].rearrange("p (m k) c -> p m k c", m=2),
+            numer[:].rearrange("p (m k) c -> p m k c", m=2),
             inv[:].unsqueeze(2).to_broadcast([P, 2, 2, CHUNKS]),
             ALU.mult,
         )
-
         rows_tab = row_banks.tile([P, NEURONS], F32, name="bank")
         rows_tb = row_banks.tile([P, NEURONS], F32, name="bank")
         for rows, k in ((rows_tab, TAB), (rows_tb, TB)):

@@ -104,6 +104,11 @@ def tile_logicgatenetwork_kernel(tc, x, w, offs, out):
         for rows, k in ((rows_tab, TAB), (rows_tb, TB)):
             for c in range(CHUNKS):
                 turn_into_row(rows[:, chunks[c]], coef[:, k, c : c + 1])
+        first_half, second_half = slice(0, PIECE), slice(PIECE, NEURONS)
+        rows_tab_copy = held.tile([P, PIECE], F32, name="rows_tab_copy")
+        nc.scalar.copy(rows_tab_copy[:], rows_tab[:, second_half])
+        rows_tb_copy = held.tile([P, PIECE], F32, name="rows_tb_copy")
+        nc.scalar.copy(rows_tb_copy[:], rows_tb[:, second_half])
 
         def per_block(name, columns):
             return [held.tile([P, columns], F32, name=f"{name}{b}") for b in range(BLOCKS)]
@@ -142,12 +147,14 @@ def tile_logicgatenetwork_kernel(tc, x, w, offs, out):
                     stop=True,
                 )
 
-        list_b = offsets[:, LIST_COLS:]
+        list_b = offsets[:, LIST_COLS : 2 * LIST_COLS]
         slope_b = per_block("slope_b", NEURONS)
-        for b in range(BLOCKS):
-            nc.vector.tensor_tensor(slope_b[b][:], a_scaled[b][:], rows_tab[:], ALU.mult)
-        for b in range(BLOCKS):
-            nc.vector.tensor_tensor(slope_b[b][:], slope_b[b][:], rows_tb[:], ALU.add)
+        nc.gpsimd.tensor_tensor(slope_b[1][:, second_half], a_scaled[1][:, second_half], rows_tab_copy[:], ALU.mult)
+        nc.gpsimd.tensor_tensor(slope_b[1][:, second_half], slope_b[1][:, second_half], rows_tb_copy[:], ALU.add)
+        nc.vector.tensor_tensor(slope_b[0][:], a_scaled[0][:], rows_tab[:], ALU.mult)
+        nc.vector.tensor_tensor(slope_b[1][:, first_half], a_scaled[1][:, first_half], rows_tab[:, first_half], ALU.mult)
+        nc.vector.tensor_tensor(slope_b[0][:], slope_b[0][:], rows_tb[:], ALU.add)
+        nc.vector.tensor_tensor(slope_b[1][:, first_half], slope_b[1][:, first_half], rows_tb[:, first_half], ALU.add)
         with_b = per_block("with_b", NEURONS)
         score = per_block("score", CLASSES)
         for b in range(BLOCKS):

@@ -149,18 +149,18 @@ def tile_logicgatenetwork_kernel(tc, x, w, offs, out):
 
         list_b = offsets[:, LIST_COLS : 2 * LIST_COLS]
         slope_b = per_block("slope_b", NEURONS)
-        nc.gpsimd.tensor_tensor(slope_b[1][:, second_half], a_scaled[1][:, second_half], rows_tab_copy[:], ALU.mult)
-        nc.gpsimd.tensor_tensor(slope_b[1][:, second_half], slope_b[1][:, second_half], rows_tb_copy[:], ALU.add)
-        nc.vector.tensor_tensor(slope_b[0][:], a_scaled[0][:], rows_tab[:], ALU.mult)
-        nc.vector.tensor_tensor(slope_b[1][:, first_half], a_scaled[1][:, first_half], rows_tab[:, first_half], ALU.mult)
-        nc.vector.tensor_tensor(slope_b[0][:], slope_b[0][:], rows_tb[:], ALU.add)
-        nc.vector.tensor_tensor(slope_b[1][:, first_half], slope_b[1][:, first_half], rows_tb[:, first_half], ALU.add)
+        nc.gpsimd.tensor_tensor(slope_b[0][:, second_half], a_scaled[0][:, second_half], rows_tab_copy[:], ALU.mult)
+        nc.gpsimd.tensor_tensor(slope_b[0][:, second_half], slope_b[0][:, second_half], rows_tb_copy[:], ALU.add)
+        nc.vector.tensor_tensor(slope_b[1][:], a_scaled[1][:], rows_tab[:], ALU.mult)
+        nc.vector.tensor_tensor(slope_b[0][:, first_half], a_scaled[0][:, first_half], rows_tab[:, first_half], ALU.mult)
+        nc.vector.tensor_tensor(slope_b[1][:], slope_b[1][:], rows_tb[:], ALU.add)
+        nc.vector.tensor_tensor(slope_b[0][:, first_half], slope_b[0][:, first_half], rows_tb[:, first_half], ALU.add)
         with_b = per_block("with_b", NEURONS)
         score = per_block("score", CLASSES)
-        for b in range(BLOCKS):
+        for b in (1, 0):
             nc.vector.tensor_tensor(with_b[b][:], signals[b][:].indirect(list_b), slope_b[b][:], ALU.mult)
-        for b in range(BLOCKS):
+        for b in (1, 0):
             nc.vector.reduce_sum(score[b][:], with_b[b][:].rearrange("p (u r) -> p u r", r=GROUP), axis=AX.X)
-        for b in range(BLOCKS):
+        for b in (1, 0):
             nc.vector.tensor_tensor(score[b][:], score[b][:], part[b][:], ALU.add)
             nc.sync.dma_start(out[b * P : (b + 1) * P, :], score[b][:])

@@ -151,16 +151,22 @@ def tile_logicgatenetwork_kernel(tc, x, w, offs, out):
         slope_b = per_block("slope_b", NEURONS)
         nc.gpsimd.tensor_tensor(slope_b[0][:, second_half], a_scaled[0][:, second_half], rows_tab_copy[:], ALU.mult)
         nc.gpsimd.tensor_tensor(slope_b[0][:, second_half], slope_b[0][:, second_half], rows_tb_copy[:], ALU.add)
-        nc.vector.tensor_tensor(slope_b[1][:], a_scaled[1][:], rows_tab[:], ALU.mult)
         nc.vector.tensor_tensor(slope_b[0][:, first_half], a_scaled[0][:, first_half], rows_tab[:, first_half], ALU.mult)
-        nc.vector.tensor_tensor(slope_b[1][:], slope_b[1][:], rows_tb[:], ALU.add)
+        nc.vector.tensor_tensor(slope_b[1][:], a_scaled[1][:], rows_tab[:], ALU.mult)
         nc.vector.tensor_tensor(slope_b[0][:, first_half], slope_b[0][:, first_half], rows_tb[:, first_half], ALU.add)
+        nc.vector.tensor_tensor(slope_b[1][:], slope_b[1][:], rows_tb[:], ALU.add)
         with_b = per_block("with_b", NEURONS)
         score = per_block("score", CLASSES)
-        for b in (1, 0):
+        for b in range(BLOCKS):
             nc.vector.tensor_tensor(with_b[b][:], signals[b][:].indirect(list_b), slope_b[b][:], ALU.mult)
-        for b in (1, 0):
-            nc.vector.reduce_sum(score[b][:], with_b[b][:].rearrange("p (u r) -> p u r", r=GROUP), axis=AX.X)
-        for b in (1, 0):
+        by_class = [with_b[b][:].rearrange("p (u r) -> p u r", r=GROUP) for b in range(BLOCKS)]
+        vector_classes, gpsimd_classes = slice(0, 3 * CLASSES // 4), slice(3 * CLASSES // 4, CLASSES)
+        pairs = held.tile([P, CLASSES // 4, 2], F32, name="pairs")
+        theirs = by_class[0][:, gpsimd_classes, :]
+        nc.gpsimd.tensor_tensor(pairs[:], theirs[:, :, 0:2], theirs[:, :, 2:4], ALU.add)
+        nc.gpsimd.tensor_tensor(score[0][:, gpsimd_classes], pairs[:, :, 0], pairs[:, :, 1], ALU.add)
+        nc.vector.reduce_sum(score[0][:, vector_classes], by_class[0][:, vector_classes, :], axis=AX.X)
+        nc.vector.reduce_sum(score[1][:], by_class[1], axis=AX.X)
+        for b in range(BLOCKS):
             nc.vector.tensor_tensor(score[b][:], score[b][:], part[b][:], ALU.add)
             nc.sync.dma_start(out[b * P : (b + 1) * P, :], score[b][:])

@@ -157,16 +157,18 @@ def tile_logicgatenetwork_kernel(tc, x, w, offs, out):
         nc.vector.tensor_tensor(slope_b[1][:], slope_b[1][:], rows_tb[:], ALU.add)
         with_b = per_block("with_b", NEURONS)
         score = per_block("score", CLASSES)
-        for b in range(BLOCKS):
-            nc.vector.tensor_tensor(with_b[b][:], signals[b][:].indirect(list_b), slope_b[b][:], ALU.mult)
         by_class = [with_b[b][:].rearrange("p (u r) -> p u r", r=GROUP) for b in range(BLOCKS)]
-        vector_classes, gpsimd_classes = slice(0, 3 * CLASSES // 4), slice(3 * CLASSES // 4, CLASSES)
-        pairs = held.tile([P, CLASSES // 4, 2], F32, name="pairs")
-        theirs = by_class[0][:, gpsimd_classes, :]
+        nc.vector.tensor_tensor(with_b[0][:], signals[0][:].indirect(list_b), slope_b[0][:], ALU.mult)
+        for half in (first_half, second_half):
+            half_list = list_b[:, half.start // 16 : half.stop // 16]
+            nc.vector.tensor_tensor(with_b[1][:, half], signals[1][:].indirect(half_list), slope_b[1][:, half], ALU.mult)
+        first_classes, second_classes = slice(0, CLASSES // 2), slice(CLASSES // 2, CLASSES)
+        pairs = held.tile([P, CLASSES // 2, 2], F32, name="pairs")
+        theirs = by_class[0][:, second_classes, :]
         nc.gpsimd.tensor_tensor(pairs[:], theirs[:, :, 0:2], theirs[:, :, 2:4], ALU.add)
-        nc.gpsimd.tensor_tensor(score[0][:, gpsimd_classes], pairs[:, :, 0], pairs[:, :, 1], ALU.add)
-        nc.vector.reduce_sum(score[0][:, vector_classes], by_class[0][:, vector_classes, :], axis=AX.X)
-        nc.vector.reduce_sum(score[1][:], by_class[1], axis=AX.X)
-        for b in range(BLOCKS):
+        nc.gpsimd.tensor_tensor(score[0][:, second_classes], pairs[:, :, 0], pairs[:, :, 1], ALU.add)
+        for b, classes in ((1, first_classes), (1, second_classes), (0, first_classes)):
+            nc.vector.reduce_sum(score[b][:, classes], by_class[b][:, classes, :], axis=AX.X)
+        for b in (1, 0):
             nc.vector.tensor_tensor(score[b][:], score[b][:], part[b][:], ALU.add)
             nc.sync.dma_start(out[b * P : (b + 1) * P, :], score[b][:])

@@ -70,35 +70,32 @@ def tile_logicgatenetwork_kernel(tc, x, w, offs, out):
             nc.tensor.transpose(bank_columns, column.to_broadcast([P, P]), ident[:])
 
         rows_denom = held.tile([P, NEURONS], F32, name="rows_denom")
-        for first in range(0, CHUNKS, 2):
+        for first, last in ((0, 1), (1, 2), (2, CHUNKS)):
             bank = row_banks.tile([P, NEURONS], F32, name="bank")
-            for i in range(2):
-                turn_into_row(bank[:, chunks[i]], denom[:, first + i : first + i + 1])
-            nc.scalar.copy(rows_denom[:, first * P : (first + 2) * P], bank[:, :PIECE])
+            for c in range(first, last):
+                turn_into_row(bank[:, chunks[c]], denom[:, c : c + 1])
+            nc.scalar.copy(rows_denom[:, first * P : last * P], bank[:, first * P : last * P])
 
         diff = held.tile([P, CHUNKS, 3, 4], F32, name="diff")
         by_four = expw[:].rearrange("p c (m r) -> p c m r", r=4)
         nc.vector.tensor_sub(diff[:, :, 0, :], by_four[:, :, :, 1], by_four[:, :, :, 2])
         nc.vector.tensor_sub(diff[:, :, 1, :], by_four[:, :, 2, :], by_four[:, :, 1, :])
+        inv = held.tile([P, 2, CHUNKS], F32, name="inv")
+        nc.vector.reciprocal(inv[:, 0, :], denom[:])
         by_bit = expw[:].rearrange("p c (i j k l) -> p c i j k l", i=2, j=2, k=2)
         nc.vector.tensor_sub(
             diff[:, :, 2, :].rearrange("p c (j l) -> p c j l", j=2), by_bit[:, :, 0, :, 1, :], by_bit[:, :, 1, :, 0, :]
         )
         numer = held.tile([P, 4, CHUNKS], F32, name="numer")
-        nc.vector.reduce_sum(numer[:, T0, :], expw[:, :, 8:], axis=AX.X)
-        inv = held.tile([P, 2, CHUNKS], F32, name="inv")
-        nc.vector.reciprocal(inv[:, 0, :], denom[:])
         nc.vector.reduce_sum(numer[:, TAB, :], diff[:, :, 0:2, :], axis=AX.XY)
         nc.vector.reduce_sum(numer[:, TB, :], diff[:, :, 1, :], axis=AX.X, negate=True)
-        nc.vector.reduce_sum(numer[:, TA, :], diff[:, :, 2, :], axis=AX.X)
         nc.vector.tensor_mul(inv[:, 1, :], inv[:, 0, :], inv[:, 0, :])
+        nc.vector.reduce_sum(numer[:, T0, :], expw[:, :, 8:], axis=AX.X)
+        nc.vector.reduce_sum(numer[:, TA, :], diff[:, :, 2, :], axis=AX.X)
         coef = held.tile([P, 4, CHUNKS], F32, name="coef")
-        nc.vector.tensor_tensor(
-            coef[:].rearrange("p (m k) c -> p m k c", m=2),
-            numer[:].rearrange("p (m k) c -> p m k c", m=2),
-            inv[:].unsqueeze(2).to_broadcast([P, 2, 2, CHUNKS]),
-            ALU.mult,
-        )
+        by_power = [tile[:].rearrange("p (m k) c -> p m k c", m=2) for tile in (coef, numer)]
+        for k in (1, 0):
+            nc.vector.tensor_mul(by_power[0][:, :, k, :], by_power[1][:, :, k, :], inv[:])
         rows_tab = row_banks.tile([P, NEURONS], F32, name="bank")
         rows_tb = row_banks.tile([P, NEURONS], F32, name="bank")
         for rows, k in ((rows_tab, TAB), (rows_tb, TB)):

import concourse.mybir as mybir
from concourse.masks import make_identity

F32 = mybir.dt.float32
U16 = mybir.dt.uint16
ALU = mybir.AluOpType
ACT = mybir.ActivationFunctionType
AX = mybir.AxisListType

P = 128
SAMPLES, SIGNALS = 256, 512
GATES, NEURONS = 16, 512
GROUP = 4
CLASSES = NEURONS // GROUP
BLOCKS = SAMPLES // P
CHUNKS = NEURONS // P
CHUNK_CLASSES = P // GROUP
LIST_COLS = NEURONS // 16
PIECE = 256
T0, TB, TA, TAB = 0, 1, 2, 3


def tile_logicgatenetwork_kernel(tc, x, w, offs, out):
    nc = tc.nc
    with (
        tc.tile_pool(name="held", bufs=1) as held,
        tc.psum_pool(name="row_banks", bufs=4) as row_banks,
        tc.psum_pool(name="turned_banks", bufs=2) as turned_banks,
        tc.psum_pool(name="first_and_last", bufs=2) as first_and_last,
    ):
        logits = held.tile([GATES * CHUNKS, P], F32, name="logits")
        nc.sync.dma_start(logits[:], w.rearrange("q (c n) -> (q c) n", c=CHUNKS))
        offsets = held.tile([P, 2 * LIST_COLS], U16, name="offsets")
        nc.sync.dma_start(offsets[:], offs)
        signals = [held.tile([P, SIGNALS], F32, name=f"signals{b}") for b in range(BLOCKS)]
        for b in range(BLOCKS):
            nc.sync.dma_start(signals[b][:], x[b * P : (b + 1) * P, :])
        warm = held.tile([P, 1], F32, name="warm")
        nc.vector.memset(warm[:], 0.0)
        nc.scalar.activation(warm[:], warm[:], ACT.Exp)

        ident = held.tile([P, P], F32, name="ident")
        make_identity(nc, ident[:])
        gates_together = held.tile([GATES * CHUNKS, CHUNKS, GATES], F32, name="gates_together")
        nc.vector.tensor_copy(
            gates_together[:], ident[: GATES * CHUNKS, : GATES * CHUNKS].rearrange("p (q c) -> p c q", c=CHUNKS)
        )
        group_of = held.tile([P, CHUNK_CLASSES], F32, name="group_of")
        nc.vector.reduce_sum(group_of[:], ident[:].rearrange("p (v r) -> p v r", r=GROUP), axis=AX.X)

        logits_t = first_and_last.tile([P, CLASSES], F32, name="bank")[:, : GATES * CHUNKS]
        nc.tensor.transpose(logits_t, logits[:], gates_together[:].rearrange("p c q -> p (c q)"))
        by_neuron = logits_t.rearrange("p (c q) -> p c q", c=CHUNKS)
        minus_top = held.tile([P, CHUNKS], F32, name="minus_top")
        nc.vector.reduce_max(minus_top[:], by_neuron, axis=AX.X, negate=True)
        expw = held.tile([P, CHUNKS, GATES], F32, name="expw")
        denom = held.tile([P, CHUNKS], F32, name="denom")
        for c in range(CHUNKS):
            nc.scalar.activation(
                expw[:, c, :],
                by_neuron[:, c, :],
                ACT.Exp,
                bias=minus_top[:, c : c + 1],
                accum_out=denom[:, c : c + 1],
            )

        chunks = [slice(c * P, (c + 1) * P) for c in range(CHUNKS)]

        def turn_into_row(bank_columns, column):
            nc.tensor.transpose(bank_columns, column.to_broadcast([P, P]), ident[:])

        rows_denom = held.tile([P, NEURONS], F32, name="rows_denom")
        for first, last in ((0, 1), (1, 2), (2, CHUNKS)):
            bank = row_banks.tile([P, NEURONS], F32, name="bank")
            for c in range(first, last):
                turn_into_row(bank[:, chunks[c]], denom[:, c : c + 1])
            nc.scalar.copy(rows_denom[:, first * P : last * P], bank[:, first * P : last * P])

        diff = held.tile([P, CHUNKS, 3, 4], F32, name="diff")
        by_four = expw[:].rearrange("p c (m r) -> p c m r", r=4)
        nc.vector.tensor_sub(diff[:, :, 0, :], by_four[:, :, :, 1], by_four[:, :, :, 2])
        nc.vector.tensor_sub(diff[:, :, 1, :], by_four[:, :, 2, :], by_four[:, :, 1, :])
        inv = held.tile([P, 2, CHUNKS], F32, name="inv")
        nc.vector.reciprocal(inv[:, 0, :], denom[:])
        by_bit = expw[:].rearrange("p c (i j k l) -> p c i j k l", i=2, j=2, k=2)
        nc.vector.tensor_sub(
            diff[:, :, 2, :].rearrange("p c (j l) -> p c j l", j=2), by_bit[:, :, 0, :, 1, :], by_bit[:, :, 1, :, 0, :]
        )
        numer = held.tile([P, 4, CHUNKS], F32, name="numer")
        nc.vector.reduce_sum(numer[:, TAB, :], diff[:, :, 0:2, :], axis=AX.XY)
        nc.vector.reduce_sum(numer[:, TB, :], diff[:, :, 1, :], axis=AX.X, negate=True)
        nc.vector.tensor_mul(inv[:, 1, :], inv[:, 0, :], inv[:, 0, :])
        nc.vector.reduce_sum(numer[:, T0, :], expw[:, :, 8:], axis=AX.X)
        nc.vector.reduce_sum(numer[:, TA, :], diff[:, :, 2, :], axis=AX.X)
        coef = held.tile([P, 4, CHUNKS], F32, name="coef")
        by_power = [tile[:].rearrange("p (m k) c -> p m k c", m=2) for tile in (coef, numer)]
        for k in (1, 0):
            nc.vector.tensor_mul(by_power[0][:, :, k, :], by_power[1][:, :, k, :], inv[:])
        rows_tab = row_banks.tile([P, NEURONS], F32, name="bank")
        rows_tb = row_banks.tile([P, NEURONS], F32, name="bank")
        for rows, k in ((rows_tab, TAB), (rows_tb, TB)):
            for c in range(CHUNKS):
                turn_into_row(rows[:, chunks[c]], coef[:, k, c : c + 1])
        first_half, second_half = slice(0, PIECE), slice(PIECE, NEURONS)
        rows_tab_copy = held.tile([P, PIECE], F32, name="rows_tab_copy")
        nc.scalar.copy(rows_tab_copy[:], rows_tab[:, second_half])
        rows_tb_copy = held.tile([P, PIECE], F32, name="rows_tb_copy")
        nc.scalar.copy(rows_tb_copy[:], rows_tb[:, second_half])

        def per_block(name, columns):
            return [held.tile([P, columns], F32, name=f"{name}{b}") for b in range(BLOCKS)]

        a_scaled = per_block("a_scaled", NEURONS)
        for b, piece in ((0, PIECE), (1, NEURONS)):
            for first in range(0, NEURONS, piece):
                nc.vector.tensor_tensor(
                    a_scaled[b][:, first : first + piece],
                    signals[b][:].indirect(offsets[:, first // 16 : (first + piece) // 16]),
                    rows_denom[:, first : first + piece],
                    ALU.mult,
                )

        part = []
        for b in range(BLOCKS):
            turned = turned_banks.tile([P, NEURONS], F32, name="bank")
            linear = held.tile([P, NEURONS], F32, name=f"linear{b}")
            for c in range(CHUNKS):
                nc.tensor.transpose(turned[:, chunks[c]], a_scaled[b][:, chunks[c]], ident[:])
            for c in range(CHUNKS):
                nc.scalar.activation(
                    linear[:, chunks[c]],
                    turned[:, chunks[c]],
                    ACT.Identity,
                    scale=coef[:, TA, c : c + 1],
                    bias=coef[:, T0, c : c + 1],
                )
            part.append(first_and_last.tile([P, CLASSES], F32, name="bank"))
            for c in range(CHUNKS):
                nc.tensor.matmul(
                    part[b][:, c * CHUNK_CLASSES : (c + 1) * CHUNK_CLASSES],
                    linear[:, chunks[c]],
                    group_of[:],
                    start=True,
                    stop=True,
                )

        list_b = offsets[:, LIST_COLS : 2 * LIST_COLS]
        slope_b = per_block("slope_b", NEURONS)
        nc.gpsimd.tensor_tensor(slope_b[0][:, second_half], a_scaled[0][:, second_half], rows_tab_copy[:], ALU.mult)
        nc.gpsimd.tensor_tensor(slope_b[0][:, second_half], slope_b[0][:, second_half], rows_tb_copy[:], ALU.add)
        nc.vector.tensor_tensor(slope_b[0][:, first_half], a_scaled[0][:, first_half], rows_tab[:, first_half], ALU.mult)
        nc.vector.tensor_tensor(slope_b[1][:], a_scaled[1][:], rows_tab[:], ALU.mult)
        nc.vector.tensor_tensor(slope_b[0][:, first_half], slope_b[0][:, first_half], rows_tb[:, first_half], ALU.add)
        nc.vector.tensor_tensor(slope_b[1][:], slope_b[1][:], rows_tb[:], ALU.add)
        with_b = per_block("with_b", NEURONS)
        score = per_block("score", CLASSES)
        by_class = [with_b[b][:].rearrange("p (u r) -> p u r", r=GROUP) for b in range(BLOCKS)]
        nc.vector.tensor_tensor(with_b[0][:], signals[0][:].indirect(list_b), slope_b[0][:], ALU.mult)
        for half in (first_half, second_half):
            half_list = list_b[:, half.start // 16 : half.stop // 16]
            nc.vector.tensor_tensor(with_b[1][:, half], signals[1][:].indirect(half_list), slope_b[1][:, half], ALU.mult)
        first_classes, second_classes = slice(0, CLASSES // 2), slice(CLASSES // 2, CLASSES)
        pairs = held.tile([P, CLASSES // 2, 2], F32, name="pairs")
        theirs = by_class[0][:, second_classes, :]
        nc.gpsimd.tensor_tensor(pairs[:], theirs[:, :, 0:2], theirs[:, :, 2:4], ALU.add)
        nc.gpsimd.tensor_tensor(score[0][:, second_classes], pairs[:, :, 0], pairs[:, :, 1], ALU.add)
        for b, classes in ((1, first_classes), (1, second_classes), (0, first_classes)):
            nc.vector.reduce_sum(score[b][:, classes], by_class[b][:, classes, :], axis=AX.X)
        for b in (1, 0):
            nc.vector.tensor_tensor(score[b][:], score[b][:], part[b][:], ALU.add)
            nc.sync.dma_start(out[b * P : (b + 1) * P, :], score[b][:])
